import numpy as np
import ml_dtypes


def mxq(x, axis, fmt="e4m3"):
    dtype, down = {"e4m3": (ml_dtypes.float8_e4m3fn, 7), "e5m2": (ml_dtypes.float8_e5m2, 14)}[fmt]
    v = np.moveaxis(np.asarray(x, np.float32).astype(ml_dtypes.bfloat16).astype(np.float64), axis, -1)
    blocks = v.reshape(v.shape[:-1] + (-1, 32))
    amax = np.abs(blocks).max(-1, keepdims=True)
    byte = np.maximum(np.where(amax > 0, np.frexp(amax)[1] - 1 + 127, 0) - down, 1)
    scale = np.exp2(byte - 127.0)
    codes = (blocks / scale).astype(np.float32).astype(dtype).astype(np.float64)
    return np.moveaxis((codes * scale).reshape(v.shape), -1, axis)


WIDE = False


def mx_kscale(k):
    if not WIDE:
        return np.ones(k)
    levels = np.array([10, -10, 5, -5, 0])
    a = np.random.permutation(np.resize(levels, k // 512 * 4)).reshape(k // 512, 4)
    idx = np.arange(k)
    return np.exp2(a[idx // 512, idx % 128 // 32])


BF16 = ml_dtypes.bfloat16


def bf(x):
    return np.asarray(x, np.float32).astype(BF16)


def f64(x):
    return np.asarray(x).astype(np.float64)


T, D, F, R = 512, 1024, 2560, 128


def silu(v):
    return v / (1.0 + np.exp(-v))


def setup_inputs():
    s = mx_kscale(D)
    return {
        "x": bf(np.random.standard_normal((T, D)) * s),
        "xa": bf(np.random.standard_normal((T, R))),
        "W_gate_up": bf(np.random.standard_normal((D, 2 * F)) / np.sqrt(D) / s[:, None]),
        "B_gate_up": bf(np.random.standard_normal((R, 2 * F)) * 0.5 / np.sqrt(R)),
        "A_down": bf(np.random.standard_normal((F, R)) / np.sqrt(F)),
    }


def reference(x, xa, W_gate_up, B_gate_up, A_down):
    gate_up = (mxq(f64(x), 1, "e4m3") @ mxq(f64(W_gate_up), 0, "e4m3")) + f64(xa) @ f64(B_gate_up)
    gate, up = gate_up[:, :F], gate_up[:, F:]
    h = silu(gate) * up
    ha = mxq(h, 1, "e4m3") @ mxq(f64(A_down), 0, "e4m3")
    return h, ha

@@ -1,0 +1,225 @@
+from contextlib import ExitStack
+
+import concourse.bass as bass
+import concourse.mybir as mybir
+import concourse.tile as tile
+from concourse.masks import make_identity
+
+F32 = mybir.dt.float32
+BF16 = mybir.dt.bfloat16
+U32 = mybir.dt.uint32
+U8 = mybir.dt.uint8
+FP8X4 = mybir.dt.float8_e4m3fn_x4
+ADD = mybir.AluOpType.add
+MULT = mybir.AluOpType.mult
+SILU = mybir.ActivationFunctionType.Silu
+
+T, D, F, R = 512, 1024, 2560, 128
+P = 128
+NT = T // P
+NG = D // 512
+CH = 512
+NCH = F // CH
+NSTEP = NCH * NT
+LOOKAHEAD = 4
+SCALAR_TILES = (1, 3)
+
+FLOPS = 2 * T * D * 2 * F + 2 * T * R * 2 * F + 2 * T * F * R
+
+
+def tile_loramlp_pa_kernel(tc, x, xa, W_gate_up, B_gate_up, A_down, out_0, out_1):
+    nc = tc.nc
+    with ExitStack() as ctx:
+        const = ctx.enter_context(tc.tile_pool(name="const", bufs=1))
+        wraw = ctx.enter_context(tc.tile_pool(name="wraw", bufs=20))
+        wgrp = ctx.enter_context(tc.tile_pool(name="wgrp", bufs=4))
+        wcod = ctx.enter_context(tc.tile_pool(name="wcod", bufs=3))
+        epi = ctx.enter_context(tc.tile_pool(name="epi", bufs=8))
+        hgp = ctx.enter_context(tc.tile_pool(name="hgp", bufs=3))
+        ps_m = ctx.enter_context(tc.psum_pool(name="ps_m", bufs=4))
+        ps_l = ctx.enter_context(tc.psum_pool(name="ps_l", bufs=2))
+        ps_t = ctx.enter_context(tc.psum_pool(name="ps_t", bufs=2))
+
+        xa_sb = const.tile([P, NT, R], BF16, name="xa_sb")
+        nc.sync.dma_start(out=xa_sb[:], in_=xa.rearrange("(i p) r -> p i r", p=P))
+        b_sb = const.tile([P, 2, F], BF16, name="b_sb")
+        b_view = B_gate_up.rearrange("r (h f) -> r h f", h=2)
+        nc.sync.dma_start(out=b_sb[:, :, 0:CH], in_=b_view[:, :, 0:CH])
+        x_sb = const.tile([P, NT * D], BF16, name="x_sb")
+        nc.sync.dma_start(
+            out=x_sb[:].rearrange("p (i k) -> p i k", i=NT),
+            in_=x.rearrange("(i p) k -> p i k", p=P),
+        )
+        raws = {}
+
+        def load_w(j):
+            for half in range(2):
+                for g in range(NG):
+                    raw = wraw.tile([P, 4, CH], BF16, name="raw", tag="raw")
+                    c0 = half * F + j * CH
+                    nc.sync.dma_start(
+                        out=raw[:],
+                        in_=W_gate_up[g * 512 : (g + 1) * 512, c0 : c0 + CH].rearrange(
+                            "(p t) c -> p t c", t=4
+                        ),
+                    )
+                    raws[(j, half, g)] = raw
+
+        load_w(0)
+        nc.sync.dma_start(out=b_sb[:, :, CH:F], in_=b_view[:, :, CH:F])
+        load_w(1)
+        a_raw = const.tile([P, NCH * 4, R], BF16, name="a_raw")
+        nc.sync.dma_start(out=a_raw[:], in_=A_down.rearrange("(n p) r -> p n r", p=P))
+        for j in range(2, NCH):
+            load_w(j)
+
+        ident_b = const.tile([P, P], BF16, name="ident_b")
+        make_identity(nc, ident_b[:])
+        ident_f = const.tile([P, P], F32, name="ident_f")
+        make_identity(nc, ident_f[:])
+
+        xat_ps = ps_t.tile([P, NT, P], BF16, name="xat_ps", tag="T")
+        for i in range(NT):
+            nc.tensor.transpose(out=xat_ps[:, i, :], in_=xa_sb[:, i, :], identity=ident_b[:])
+        xat = const.tile([P, NT, P], BF16, name="xat")
+        nc.vector.tensor_copy(out=xat[:], in_=xat_ps[:])
+
+        x_words = x_sb[:].bitcast(F32).rearrange("p (i g q u) -> p i g u q", i=NT, g=NG, u=2)
+        xg = const.tile([P, NG * T * 4], BF16, name="xg", align_bytes=64)
+        xg_words = xg[:].bitcast(F32).rearrange("p (g t u) -> p g t u", g=NG, u=2)
+        for i in range(NT):
+            xt = ps_t.tile([P, NG, 2, P], F32, name="xt", tag="T")
+            for g in range(NG):
+                for u in range(2):
+                    nc.tensor.transpose(out=xt[:, g, u, :], in_=x_words[:, i, g, u, :], identity=ident_f[:])
+            eng_copy = nc.scalar.copy if i % 2 == 0 else nc.vector.tensor_copy
+            eng_copy(
+                out=xg_words[:, :, i * P : (i + 1) * P, :],
+                in_=xt[:].rearrange("p g u t -> p g t u"),
+            )
+        xc = const.tile([P, NG * T], U32, name="xc", align_bytes=64)
+        xs = const.tile([P, NG * T], U8, name="xs", align_bytes=64)
+        nc.vector.quantize_mx(out=xc[:].bitcast(FP8X4), scales=xs[:], in_=xg[:])
+
+        etiles = {}
+        wcodes = {}
+
+        def lora(s):
+            j, i = divmod(s, NT)
+            e = epi.tile([P, 2, CH], F32, name="e", tag="e")
+            etiles[s] = e
+            for half in range(2):
+                lp = ps_l.tile([P, CH], F32, name="lp", tag="L")
+                nc.tensor.matmul(
+                    out=lp[:],
+                    lhsT=xat[:, i, :],
+                    rhs=b_sb[:, half, j * CH : (j + 1) * CH],
+                    start=True,
+                    stop=True,
+                )
+                nc.scalar.copy(out=e[:, half, :], in_=lp[:])
+
+        def wprep(j, n):
+            half, g = divmod(n, NG)
+            if n == 0:
+                wc_new = wcod.tile([P, 2, NG, CH], U32, name="wc", tag="wc", align_bytes=64)
+                ws_new = wcod.tile([P, 2, NG, CH], U8, name="ws", tag="ws", align_bytes=64)
+                wcodes[j] = (wc_new, ws_new)
+            wc, ws = wcodes[j]
+            raw = raws[(j, half, g)]
+            grp = wgrp.tile([P, 4 * CH], BF16, name="grp", tag="grp", align_bytes=64)
+            dst = grp[:].rearrange("p (c i t) -> p c t i", i=4, t=4)
+            src = raw[:].rearrange("p t (c i) -> p c t i", i=4)
+            if (j * 4 + n) % 5 in SCALAR_TILES:
+                nc.scalar.copy(out=dst, in_=src)
+            else:
+                nc.vector.tensor_copy(out=dst, in_=src)
+            nc.vector.quantize_mx(
+                out=wc[:, half, g, :].bitcast(FP8X4), scales=ws[:, half, g, :], in_=grp[:]
+            )
+
+        hc = const.tile([P, NCH * T], U32, name="hc", align_bytes=64)
+        hs = const.tile([P, NCH * T], U8, name="hs", align_bytes=64)
+
+        def main(s):
+            j, i = divmod(s, NT)
+            e = etiles[s]
+            wc, ws = wcodes[j]
+            ms = []
+            for half in range(2):
+                m = ps_m.tile([P, CH], F32, name="m", tag="M")
+                for g in range(NG):
+                    cols = slice(g * T + i * P, g * T + (i + 1) * P)
+                    nc.tensor.matmul_mx(
+                        out=m[:],
+                        lhsT=xc[:, cols].bitcast(FP8X4),
+                        lhsT_scale=xs[:, cols],
+                        rhs=wc[:, half, g, :].bitcast(FP8X4),
+                        rhs_scale=ws[:, half, g, :],
+                        start=(g == 0),
+                        stop=(g == NG - 1),
+                    )
+                ms.append(m)
+            nc.vector.tensor_tensor(out=e[:, 0, :], in0=ms[0][:], in1=e[:, 0, :], op=ADD)
+            nc.scalar.activation(out=e[:, 0, :], in_=e[:, 0, :], func=SILU)
+            nc.vector.tensor_tensor(out=e[:, 1, :], in0=ms[1][:], in1=e[:, 1, :], op=ADD)
+            nc.vector.tensor_tensor(out=e[:, 1, :], in0=e[:, 0, :], in1=e[:, 1, :], op=MULT)
+            store = nc.sync if j == NCH - 1 else nc.gpsimd
+            store.dma_start(out=out_0[i * P : (i + 1) * P, j * CH : (j + 1) * CH], in_=e[:, 1, :])
+            ht = ps_t.tile([P, 4, P], F32, name="ht", tag="T")
+            for q in range(4):
+                nc.tensor.transpose(out=ht[:, q, :], in_=e[:, 1, q * P : (q + 1) * P], identity=ident_f[:])
+            hg = hgp.tile([P, P, 4], BF16, name="hg", tag="hg", align_bytes=64)
+            nc.scalar.copy(out=hg[:], in_=ht[:].rearrange("p q t -> p t q"))
+            cols = slice(j * T + i * P, j * T + (i + 1) * P)
+            nc.vector.quantize_mx(
+                out=hc[:, cols].bitcast(FP8X4),
+                scales=hs[:, cols],
+                in_=hg[:].rearrange("p t q -> p (t q)"),
+            )
+
+        for s in range(LOOKAHEAD):
+            lora(s)
+        for n in range(4):
+            wprep(0, n)
+
+        a_grp = const.tile([P, NCH * R * 4], BF16, name="a_grp", align_bytes=64)
+        ac = const.tile([P, NCH * R], U32, name="ac", align_bytes=64)
+        a_s = const.tile([P, NCH * R], U8, name="a_s", align_bytes=64)
+
+        for s in range(NSTEP):
+            j, i = divmod(s, NT)
+            if j + 1 < NCH:
+                wprep(j + 1, i)
+            if s + LOOKAHEAD < NSTEP:
+                lora(s + LOOKAHEAD)
+            main(s)
+            if s == 5:
+                nc.vector.tensor_copy(
+                    out=a_grp[:].rearrange("p (g r t) -> p g r t", g=NCH, t=4),
+                    in_=a_raw[:].rearrange("p (g t) r -> p g r t", t=4),
+                )
+            if s == 6:
+                nc.vector.quantize_mx(
+                    out=ac[:, 0:512].bitcast(FP8X4), scales=a_s[:, 0:512], in_=a_grp[:, 0:2048]
+                )
+                nc.vector.quantize_mx(
+                    out=ac[:, 512:640].bitcast(FP8X4), scales=a_s[:, 512:640], in_=a_grp[:, 2048:2560]
+                )
+
+        ha_ps = ps_t.tile([P, NT, R], F32, name="ha_ps", tag="T")
+        ha_sb = const.tile([P, NT, R], F32, name="ha_sb")
+        for i in range(NT):
+            for j in range(NCH):
+                cols = slice(j * T + i * P, j * T + (i + 1) * P)
+                nc.tensor.matmul_mx(
+                    out=ha_ps[:, i, :],
+                    lhsT=hc[:, cols].bitcast(FP8X4),
+                    lhsT_scale=hs[:, cols],
+                    rhs=ac[:, j * R : (j + 1) * R].bitcast(FP8X4),
+                    rhs_scale=a_s[:, j * R : (j + 1) * R],
+                    start=(j == 0),
+                    stop=(j == NCH - 1),
+                )
+        nc.scalar.copy(out=ha_sb[:], in_=ha_ps[:])
+        nc.sync.dma_start(out=out_1.rearrange("(i p) r -> p i r", p=P), in_=ha_sb[:])

@@ -1,8 +1,6 @@
 from contextlib import ExitStack
 
-import concourse.bass as bass
 import concourse.mybir as mybir
-import concourse.tile as tile
 from concourse.masks import make_identity
 
 F32 = mybir.dt.float32
@@ -21,8 +19,11 @@ NG = D // 512
 CH = 512
 NCH = F // CH
 NSTEP = NCH * NT
-LOOKAHEAD = 4
-SCALAR_TILES = (1, 3)
+NTILE = NCH * 2 * NG
+RAW_BUFS = 12
+VCOLS_FIRST = {0: 512, 1: 512, 2: 320, 3: 320}
+VCOLS = 384
+GPSIMD_MUL_STEPS = 18
 
 FLOPS = 2 * T * D * 2 * F + 2 * T * R * 2 * F + 2 * T * F * R
 
@@ -31,83 +32,96 @@ def tile_loramlp_pa_kernel(tc, x, xa, W_gate_up, B_gate_up, A_down, out_0, out_1
     nc = tc.nc
     with ExitStack() as ctx:
         const = ctx.enter_context(tc.tile_pool(name="const", bufs=1))
-        wraw = ctx.enter_context(tc.tile_pool(name="wraw", bufs=20))
+        wraw = ctx.enter_context(tc.tile_pool(name="wraw", bufs=RAW_BUFS))
         wgrp = ctx.enter_context(tc.tile_pool(name="wgrp", bufs=4))
         wcod = ctx.enter_context(tc.tile_pool(name="wcod", bufs=3))
-        epi = ctx.enter_context(tc.tile_pool(name="epi", bufs=8))
+        epi = ctx.enter_context(tc.tile_pool(name="epi", bufs=12))
         hgp = ctx.enter_context(tc.tile_pool(name="hgp", bufs=3))
         ps_m = ctx.enter_context(tc.psum_pool(name="ps_m", bufs=4))
         ps_l = ctx.enter_context(tc.psum_pool(name="ps_l", bufs=2))
         ps_t = ctx.enter_context(tc.psum_pool(name="ps_t", bufs=2))
+        ctx.enter_context(tc.manual_schedule())
+
+        raws = {}
+        grps = {}
+        wcodes = {}
+        etiles = {}
+        lps = {}
+        mps = {}
+        hts = {}
+        hgs = {}
+
+        def load_w(m):
+            j, n = divmod(m, 2 * NG)
+            half, g = divmod(n, NG)
+            raw = wraw.tile([P, 4, CH], BF16, name="raw", tag="raw")
+            c0 = half * F + j * CH
+            nc.sync.dma_start(
+                out=raw[:],
+                in_=W_gate_up[g * 512 : (g + 1) * 512, c0 : c0 + CH].rearrange("(p t) c -> p t c", t=4),
+            )
+            raws[m] = raw
 
         xa_sb = const.tile([P, NT, R], BF16, name="xa_sb")
         nc.sync.dma_start(out=xa_sb[:], in_=xa.rearrange("(i p) r -> p i r", p=P))
         b_sb = const.tile([P, 2, F], BF16, name="b_sb")
         b_view = B_gate_up.rearrange("r (h f) -> r h f", h=2)
         nc.sync.dma_start(out=b_sb[:, :, 0:CH], in_=b_view[:, :, 0:CH])
-        x_sb = const.tile([P, NT * D], BF16, name="x_sb")
-        nc.sync.dma_start(
-            out=x_sb[:].rearrange("p (i k) -> p i k", i=NT),
-            in_=x.rearrange("(i p) k -> p i k", p=P),
-        )
-        raws = {}
-
-        def load_w(j):
-            for half in range(2):
-                for g in range(NG):
-                    raw = wraw.tile([P, 4, CH], BF16, name="raw", tag="raw")
-                    c0 = half * F + j * CH
-                    nc.sync.dma_start(
-                        out=raw[:],
-                        in_=W_gate_up[g * 512 : (g + 1) * 512, c0 : c0 + CH].rearrange(
-                            "(p t) c -> p t c", t=4
-                        ),
-                    )
-                    raws[(j, half, g)] = raw
-
         load_w(0)
-        nc.sync.dma_start(out=b_sb[:, :, CH:F], in_=b_view[:, :, CH:F])
         load_w(1)
+        x_sb = const.tile([P, NT * D], BF16, name="x_sb")
+        for i in range(NT):
+            nc.sync.dma_start(out=x_sb[:, i * D : (i + 1) * D], in_=x[i * P : (i + 1) * P, :])
+        load_w(2)
+        load_w(3)
+        nc.sync.dma_start(out=b_sb[:, :, CH:F], in_=b_view[:, :, CH:F])
+        for m in range(4, 8):
+            load_w(m)
         a_raw = const.tile([P, NCH * 4, R], BF16, name="a_raw")
         nc.sync.dma_start(out=a_raw[:], in_=A_down.rearrange("(n p) r -> p n r", p=P))
-        for j in range(2, NCH):
-            load_w(j)
+        for m in range(8, RAW_BUFS):
+            load_w(m)
 
         ident_b = const.tile([P, P], BF16, name="ident_b")
         make_identity(nc, ident_b[:])
         ident_f = const.tile([P, P], F32, name="ident_f")
         make_identity(nc, ident_f[:])
 
-        xat_ps = ps_t.tile([P, NT, P], BF16, name="xat_ps", tag="T")
-        for i in range(NT):
-            nc.tensor.transpose(out=xat_ps[:, i, :], in_=xa_sb[:, i, :], identity=ident_b[:])
         xat = const.tile([P, NT, P], BF16, name="xat")
-        nc.vector.tensor_copy(out=xat[:], in_=xat_ps[:])
+        xg = const.tile([P, NT * NG * P * 4], BF16, name="xg", align_bytes=64)
+        xc = const.tile([P, NT * NG * P], U32, name="xc", align_bytes=64)
+        xs = const.tile([P, NT * NG * P], U8, name="xs", align_bytes=64)
+        hc = const.tile([P, NCH * T], U32, name="hc", align_bytes=64)
+        hs = const.tile([P, NCH * T], U8, name="hs", align_bytes=64)
+        a_grp = const.tile([P, NCH * R * 4], BF16, name="a_grp", align_bytes=64)
+        ac = const.tile([P, NCH * R], U32, name="ac", align_bytes=64)
+        a_s = const.tile([P, NCH * R], U8, name="a_s", align_bytes=64)
+        ha_sb = const.tile([P, NT, R], F32, name="ha_sb")
 
         x_words = x_sb[:].bitcast(F32).rearrange("p (i g q u) -> p i g u q", i=NT, g=NG, u=2)
-        xg = const.tile([P, NG * T * 4], BF16, name="xg", align_bytes=64)
-        xg_words = xg[:].bitcast(F32).rearrange("p (g t u) -> p g t u", g=NG, u=2)
-        for i in range(NT):
+        xg_words = xg[:].bitcast(F32).rearrange("p (i g t u) -> p i g t u", i=NT, g=NG, u=2)
+
+        def x_transpose(i):
             xt = ps_t.tile([P, NG, 2, P], F32, name="xt", tag="T")
             for g in range(NG):
                 for u in range(2):
                     nc.tensor.transpose(out=xt[:, g, u, :], in_=x_words[:, i, g, u, :], identity=ident_f[:])
-            eng_copy = nc.scalar.copy if i % 2 == 0 else nc.vector.tensor_copy
-            eng_copy(
-                out=xg_words[:, :, i * P : (i + 1) * P, :],
-                in_=xt[:].rearrange("p g u t -> p g t u"),
+            return xt
+
+        def x_copy(i, xt, copy):
+            copy(out=xg_words[:, i, :, :, :], in_=xt[:].rearrange("p g u t -> p g t u"))
+
+        def x_quant(i):
+            w = NG * P
+            nc.vector.quantize_mx(
+                out=xc[:, i * w : (i + 1) * w].bitcast(FP8X4),
+                scales=xs[:, i * w : (i + 1) * w],
+                in_=xg[:, i * w * 4 : (i + 1) * w * 4],
             )
-        xc = const.tile([P, NG * T], U32, name="xc", align_bytes=64)
-        xs = const.tile([P, NG * T], U8, name="xs", align_bytes=64)
-        nc.vector.quantize_mx(out=xc[:].bitcast(FP8X4), scales=xs[:], in_=xg[:])
 
-        etiles = {}
-        wcodes = {}
-
-        def lora(s):
+        def lora_mm(s):
             j, i = divmod(s, NT)
-            e = epi.tile([P, 2, CH], F32, name="e", tag="e")
-            etiles[s] = e
+            lps[s] = []
             for half in range(2):
                 lp = ps_l.tile([P, CH], F32, name="lp", tag="L")
                 nc.tensor.matmul(
@@ -117,41 +131,46 @@ def tile_loramlp_pa_kernel(tc, x, xa, W_gate_up, B_gate_up, A_down, out_0, out_1
                     start=True,
                     stop=True,
                 )
-                nc.scalar.copy(out=e[:, half, :], in_=lp[:])
+                lps[s].append(lp)
 
-        def wprep(j, n):
+        def lora_copy(s, half):
+            if half == 0:
+                e_new = epi.tile([P, 2, CH], F32, name="e", tag="e")
+                etiles[s] = e_new
+            nc.scalar.copy(out=etiles[s][:, half, :], in_=lps[s][half][:])
+
+        def regroup(m):
+            grp = wgrp.tile([P, 4 * CH], BF16, name="grp", tag="grp", align_bytes=64)
+            grps[m] = grp
+            dst = grp[:].rearrange("p (c i t) -> p c t i", i=4, t=4)
+            src = raws[m][:].rearrange("p t (c i) -> p c t i", i=4)
+            vq = VCOLS_FIRST.get(m, VCOLS) // 4
+            nc.vector.tensor_copy(out=dst[:, 0:vq], in_=src[:, 0:vq])
+            if vq < CH // 4:
+                nc.scalar.copy(out=dst[:, vq : CH // 4], in_=src[:, vq : CH // 4])
+
+        def w_quant(m):
+            j, n = divmod(m, 2 * NG)
             half, g = divmod(n, NG)
             if n == 0:
                 wc_new = wcod.tile([P, 2, NG, CH], U32, name="wc", tag="wc", align_bytes=64)
                 ws_new = wcod.tile([P, 2, NG, CH], U8, name="ws", tag="ws", align_bytes=64)
                 wcodes[j] = (wc_new, ws_new)
             wc, ws = wcodes[j]
-            raw = raws[(j, half, g)]
-            grp = wgrp.tile([P, 4 * CH], BF16, name="grp", tag="grp", align_bytes=64)
-            dst = grp[:].rearrange("p (c i t) -> p c t i", i=4, t=4)
-            src = raw[:].rearrange("p t (c i) -> p c t i", i=4)
-            if (j * 4 + n) % 5 in SCALAR_TILES:
-                nc.scalar.copy(out=dst, in_=src)
-            else:
-                nc.vector.tensor_copy(out=dst, in_=src)
             nc.vector.quantize_mx(
-                out=wc[:, half, g, :].bitcast(FP8X4), scales=ws[:, half, g, :], in_=grp[:]
+                out=wc[:, half, g, :].bitcast(FP8X4), scales=ws[:, half, g, :], in_=grps[m][:]
             )
 
-        hc = const.tile([P, NCH * T], U32, name="hc", align_bytes=64)
-        hs = const.tile([P, NCH * T], U8, name="hs", align_bytes=64)
-
-        def main(s):
+        def mx(s):
             j, i = divmod(s, NT)
-            e = etiles[s]
             wc, ws = wcodes[j]
-            ms = []
+            mps[s] = []
             for half in range(2):
-                m = ps_m.tile([P, CH], F32, name="m", tag="M")
+                mp = ps_m.tile([P, CH], F32, name="mp", tag="M")
                 for g in range(NG):
-                    cols = slice(g * T + i * P, g * T + (i + 1) * P)
+                    cols = slice((i * NG + g) * P, (i * NG + g + 1) * P)
                     nc.tensor.matmul_mx(
-                        out=m[:],
+                        out=mp[:],
                         lhsT=xc[:, cols].bitcast(FP8X4),
                         lhsT_scale=xs[:, cols],
                         rhs=wc[:, half, g, :].bitcast(FP8X4),
@@ -159,61 +178,68 @@ def tile_loramlp_pa_kernel(tc, x, xa, W_gate_up, B_gate_up, A_down, out_0, out_1
                         start=(g == 0),
                         stop=(g == NG - 1),
                     )
-                ms.append(m)
-            nc.vector.tensor_tensor(out=e[:, 0, :], in0=ms[0][:], in1=e[:, 0, :], op=ADD)
+                mps[s].append(mp)
+
+        def add(s, half):
+            e = etiles[s]
+            nc.vector.tensor_tensor(out=e[:, half, :], in0=mps[s][half][:], in1=e[:, half, :], op=ADD)
+
+        def silu(s):
+            e = etiles[s]
             nc.scalar.activation(out=e[:, 0, :], in_=e[:, 0, :], func=SILU)
-            nc.vector.tensor_tensor(out=e[:, 1, :], in0=ms[1][:], in1=e[:, 1, :], op=ADD)
-            nc.vector.tensor_tensor(out=e[:, 1, :], in0=e[:, 0, :], in1=e[:, 1, :], op=MULT)
-            store = nc.sync if j == NCH - 1 else nc.gpsimd
-            store.dma_start(out=out_0[i * P : (i + 1) * P, j * CH : (j + 1) * CH], in_=e[:, 1, :])
+
+        def mul(s):
+            e = etiles[s]
+            eng = nc.gpsimd if s < GPSIMD_MUL_STEPS else nc.vector
+            eng.tensor_tensor(out=e[:, 1, :], in0=e[:, 0, :], in1=e[:, 1, :], op=MULT)
+
+        def store(s):
+            j, i = divmod(s, NT)
+            nc.sync.dma_start(
+                out=out_0[i * P : (i + 1) * P, j * CH : (j + 1) * CH], in_=etiles[s][:, 1, :]
+            )
+
+        def h_transpose(s):
             ht = ps_t.tile([P, 4, P], F32, name="ht", tag="T")
             for q in range(4):
-                nc.tensor.transpose(out=ht[:, q, :], in_=e[:, 1, q * P : (q + 1) * P], identity=ident_f[:])
+                nc.tensor.transpose(
+                    out=ht[:, q, :], in_=etiles[s][:, 1, q * P : (q + 1) * P], identity=ident_f[:]
+                )
+            hts[s] = ht
+
+        def h_copy(s):
             hg = hgp.tile([P, P, 4], BF16, name="hg", tag="hg", align_bytes=64)
-            nc.scalar.copy(out=hg[:], in_=ht[:].rearrange("p q t -> p t q"))
+            nc.scalar.copy(out=hg[:], in_=hts[s][:].rearrange("p q t -> p t q"))
+            hgs[s] = hg
+
+        def h_quant(s):
+            j, i = divmod(s, NT)
             cols = slice(j * T + i * P, j * T + (i + 1) * P)
             nc.vector.quantize_mx(
                 out=hc[:, cols].bitcast(FP8X4),
                 scales=hs[:, cols],
-                in_=hg[:].rearrange("p t q -> p (t q)"),
+                in_=hgs[s][:].rearrange("p t q -> p (t q)"),
             )
 
-        for s in range(LOOKAHEAD):
-            lora(s)
-        for n in range(4):
-            wprep(0, n)
+        def a_regroup(g):
+            nc.vector.tensor_copy(
+                out=a_grp[:, g * R * 4 : (g + 1) * R * 4].rearrange("p (r t) -> p r t", t=4),
+                in_=a_raw[:, g * 4 : (g + 1) * 4, :].rearrange("p t r -> p r t"),
+            )
 
-        a_grp = const.tile([P, NCH * R * 4], BF16, name="a_grp", align_bytes=64)
-        ac = const.tile([P, NCH * R], U32, name="ac", align_bytes=64)
-        a_s = const.tile([P, NCH * R], U8, name="a_s", align_bytes=64)
+        def a_quant(g):
+            nc.vector.quantize_mx(
+                out=ac[:, g * R : (g + 1) * R].bitcast(FP8X4),
+                scales=a_s[:, g * R : (g + 1) * R],
+                in_=a_grp[:, g * R * 4 : (g + 1) * R * 4],
+            )
 
-        for s in range(NSTEP):
-            j, i = divmod(s, NT)
-            if j + 1 < NCH:
-                wprep(j + 1, i)
-            if s + LOOKAHEAD < NSTEP:
-                lora(s + LOOKAHEAD)
-            main(s)
-            if s == 5:
-                nc.vector.tensor_copy(
-                    out=a_grp[:].rearrange("p (g r t) -> p g r t", g=NCH, t=4),
-                    in_=a_raw[:].rearrange("p (g t) r -> p g r t", t=4),
-                )
-            if s == 6:
-                nc.vector.quantize_mx(
-                    out=ac[:, 0:512].bitcast(FP8X4), scales=a_s[:, 0:512], in_=a_grp[:, 0:2048]
-                )
-                nc.vector.quantize_mx(
-                    out=ac[:, 512:640].bitcast(FP8X4), scales=a_s[:, 512:640], in_=a_grp[:, 2048:2560]
-                )
-
-        ha_ps = ps_t.tile([P, NT, R], F32, name="ha_ps", tag="T")
-        ha_sb = const.tile([P, NT, R], F32, name="ha_sb")
-        for i in range(NT):
+        def second(i):
+            ha_ps = ps_m.tile([P, R], F32, name="ha_ps", tag="M")
             for j in range(NCH):
                 cols = slice(j * T + i * P, j * T + (i + 1) * P)
                 nc.tensor.matmul_mx(
-                    out=ha_ps[:, i, :],
+                    out=ha_ps[:],
                     lhsT=hc[:, cols].bitcast(FP8X4),
                     lhsT_scale=hs[:, cols],
                     rhs=ac[:, j * R : (j + 1) * R].bitcast(FP8X4),
@@ -221,5 +247,73 @@ def tile_loramlp_pa_kernel(tc, x, xa, W_gate_up, B_gate_up, A_down, out_0, out_1
                     start=(j == 0),
                     stop=(j == NCH - 1),
                 )
-        nc.scalar.copy(out=ha_sb[:], in_=ha_ps[:])
-        nc.sync.dma_start(out=out_1.rearrange("(i p) r -> p i r", p=P), in_=ha_sb[:])
+            nc.scalar.copy(out=ha_sb[:, i, :], in_=ha_ps[:])
+            nc.sync.dma_start(out=out_1[i * P : (i + 1) * P, :], in_=ha_sb[:, i, :])
+
+        xat_ps = ps_t.tile([P, NT, P], BF16, name="xat_ps", tag="T")
+        for i in range(NT):
+            nc.tensor.transpose(out=xat_ps[:, i, :], in_=xa_sb[:, i, :], identity=ident_b[:])
+        nc.vector.tensor_copy(out=xat[:], in_=xat_ps[:])
+        for s in range(4):
+            lora_mm(s)
+            lora_copy(s, 0)
+            lora_copy(s, 1)
+            if s == 1:
+                regroup(0)
+            if s == 2:
+                regroup(1)
+        w_quant(0)
+        w_quant(1)
+        x_copy(0, x_transpose(0), nc.vector.tensor_copy)
+        x_copy(1, x_transpose(1), nc.scalar.copy)
+        regroup(2)
+        x_quant(0)
+        x_copy(2, x_transpose(2), nc.scalar.copy)
+        x_copy(3, x_transpose(3), nc.scalar.copy)
+        regroup(3)
+        w_quant(2)
+        x_quant(1)
+        w_quant(3)
+        x_quant(2)
+        x_quant(3)
+        for m in range(RAW_BUFS, RAW_BUFS + 4):
+            load_w(m)
+
+        for tick in range(-2, NSTEP + 4):
+            if 0 <= tick - 2 < NSTEP:
+                h_transpose(tick - 2)
+            if 0 <= tick + 1 < NSTEP:
+                mx(tick + 1)
+            if 0 <= tick < NSTEP:
+                add(tick, 0)
+                add(tick, 1)
+            if 4 <= tick + 3 < NSTEP:
+                lora_copy(tick + 3, 0)
+            if 0 <= tick < NSTEP:
+                silu(tick)
+            if 4 <= tick + 3 < NSTEP:
+                lora_copy(tick + 3, 1)
+            if 4 <= tick + 4 < NSTEP:
+                lora_mm(tick + 4)
+            if 0 <= tick - 1 < NSTEP:
+                mul(tick - 1)
+                if tick - 1 >= GPSIMD_MUL_STEPS:
+                    store(tick - 1)
+            if 0 <= tick - 2 < GPSIMD_MUL_STEPS:
+                store(tick - 2)
+            if 0 <= tick - 2 < NSTEP:
+                h_copy(tick - 2)
+            if 0 <= tick - 3 < NSTEP:
+                h_quant(tick - 3)
+            if 4 <= tick + 5 < NTILE:
+                w_quant(tick + 5)
+            if 4 <= tick + 6 < NTILE:
+                regroup(tick + 6)
+            if RAW_BUFS + 4 <= tick + 17 < NTILE:
+                load_w(tick + 17)
+            if 0 <= tick - 4 < NCH:
+                a_regroup(tick - 4)
+            if 0 <= tick - 5 < NCH:
+                a_quant(tick - 5)
+            if 0 <= tick - 3 - (NSTEP - NT) < NT:
+                second(tick - 3 - (NSTEP - NT))

@@ -8,7 +8,6 @@ BF16 = mybir.dt.bfloat16
 U32 = mybir.dt.uint32
 U8 = mybir.dt.uint8
 FP8X4 = mybir.dt.float8_e4m3fn_x4
-ADD = mybir.AluOpType.add
 MULT = mybir.AluOpType.mult
 SILU = mybir.ActivationFunctionType.Silu
 
@@ -18,12 +17,13 @@ NT = T // P
 NG = D // 512
 CH = 512
 NCH = F // CH
-NSTEP = NCH * NT
+NUNIT = NCH * 2
 NTILE = NCH * 2 * NG
 RAW_BUFS = 12
-VCOLS_FIRST = {0: 512, 1: 512, 2: 320, 3: 320}
-VCOLS = 384
-GPSIMD_MUL_STEPS = 18
+EARLY_TILES = 8
+VCOLS_EARLY = 320
+VCOLS = 512
+V_EVAC_FROM = 7
 
 FLOPS = 2 * T * D * 2 * F + 2 * T * R * 2 * F + 2 * T * F * R
 
@@ -35,19 +35,20 @@ def tile_loramlp_pa_kernel(tc, x, xa, W_gate_up, B_gate_up, A_down, out_0, out_1
         wraw = ctx.enter_context(tc.tile_pool(name="wraw", bufs=RAW_BUFS))
         wgrp = ctx.enter_context(tc.tile_pool(name="wgrp", bufs=4))
         wcod = ctx.enter_context(tc.tile_pool(name="wcod", bufs=3))
-        epi = ctx.enter_context(tc.tile_pool(name="epi", bufs=12))
-        hgp = ctx.enter_context(tc.tile_pool(name="hgp", bufs=3))
-        ps_m = ctx.enter_context(tc.psum_pool(name="ps_m", bufs=4))
-        ps_l = ctx.enter_context(tc.psum_pool(name="ps_l", bufs=2))
+        msp = ctx.enter_context(tc.tile_pool(name="msp", bufs=8))
+        epi = ctx.enter_context(tc.tile_pool(name="epi", bufs=8))
+        hgp = ctx.enter_context(tc.tile_pool(name="hgp", bufs=4))
+        ps_m = ctx.enter_context(tc.psum_pool(name="ps_m", bufs=6))
         ps_t = ctx.enter_context(tc.psum_pool(name="ps_t", bufs=2))
         ctx.enter_context(tc.manual_schedule())
 
         raws = {}
         grps = {}
         wcodes = {}
+        mts = {}
+        msbs = {}
+        gus = {}
         etiles = {}
-        lps = {}
-        mps = {}
         hts = {}
         hgs = {}
 
@@ -62,30 +63,36 @@ def tile_loramlp_pa_kernel(tc, x, xa, W_gate_up, B_gate_up, A_down, out_0, out_1
             )
             raws[m] = raw
 
+        x_sb = const.tile([P, NT * D], BF16, name="x_sb")
+
+        def load_x(i):
+            nc.sync.dma_start(out=x_sb[:, i * D : (i + 1) * D], in_=x[i * P : (i + 1) * P, :])
+
+        load_x(0)
+        load_x(1)
+        load_w(0)
+        load_w(1)
         xa_sb = const.tile([P, NT, R], BF16, name="xa_sb")
         nc.sync.dma_start(out=xa_sb[:], in_=xa.rearrange("(i p) r -> p i r", p=P))
         b_sb = const.tile([P, 2, F], BF16, name="b_sb")
         b_view = B_gate_up.rearrange("r (h f) -> r h f", h=2)
-        nc.sync.dma_start(out=b_sb[:, :, 0:CH], in_=b_view[:, :, 0:CH])
-        load_w(0)
-        load_w(1)
-        x_sb = const.tile([P, NT * D], BF16, name="x_sb")
-        for i in range(NT):
-            nc.sync.dma_start(out=x_sb[:, i * D : (i + 1) * D], in_=x[i * P : (i + 1) * P, :])
         load_w(2)
         load_w(3)
-        nc.sync.dma_start(out=b_sb[:, :, CH:F], in_=b_view[:, :, CH:F])
+        load_x(2)
+        load_x(3)
+        nc.sync.dma_start(out=b_sb[:, :, 0:CH], in_=b_view[:, :, 0:CH])
         for m in range(4, 8):
+            load_w(m)
+        nc.sync.dma_start(out=b_sb[:, :, CH:F], in_=b_view[:, :, CH:F])
+        for m in range(8, RAW_BUFS):
             load_w(m)
         a_raw = const.tile([P, NCH * 4, R], BF16, name="a_raw")
         nc.sync.dma_start(out=a_raw[:], in_=A_down.rearrange("(n p) r -> p n r", p=P))
-        for m in range(8, RAW_BUFS):
-            load_w(m)
 
-        ident_b = const.tile([P, P], BF16, name="ident_b")
-        make_identity(nc, ident_b[:])
         ident_f = const.tile([P, P], F32, name="ident_f")
         make_identity(nc, ident_f[:])
+        ident_b = const.tile([P, P], BF16, name="ident_b")
+        make_identity(nc, ident_b[:])
 
         xat = const.tile([P, NT, P], BF16, name="xat")
         xg = const.tile([P, NT * NG * P * 4], BF16, name="xg", align_bytes=64)
@@ -99,7 +106,7 @@ def tile_loramlp_pa_kernel(tc, x, xa, W_gate_up, B_gate_up, A_down, out_0, out_1
         ha_sb = const.tile([P, NT, R], F32, name="ha_sb")
 
         x_words = x_sb[:].bitcast(F32).rearrange("p (i g q u) -> p i g u q", i=NT, g=NG, u=2)
-        xg_words = xg[:].bitcast(F32).rearrange("p (i g t u) -> p i g t u", i=NT, g=NG, u=2)
+        xg_words = xg[:].bitcast(F32).rearrange("p (a g b t u) -> p a b g t u", a=2, g=NG, b=2, u=2)
 
         def x_transpose(i):
             xt = ps_t.tile([P, NG, 2, P], F32, name="xt", tag="T")
@@ -109,45 +116,27 @@ def tile_loramlp_pa_kernel(tc, x, xa, W_gate_up, B_gate_up, A_down, out_0, out_1
             return xt
 
         def x_copy(i, xt, copy):
-            copy(out=xg_words[:, i, :, :, :], in_=xt[:].rearrange("p g u t -> p g t u"))
+            copy(out=xg_words[:, i // 2, i % 2, :, :, :], in_=xt[:].rearrange("p g u t -> p g t u"))
 
-        def x_quant(i):
-            w = NG * P
+        def x_quant(a):
+            w = NG * 2 * P
             nc.vector.quantize_mx(
-                out=xc[:, i * w : (i + 1) * w].bitcast(FP8X4),
-                scales=xs[:, i * w : (i + 1) * w],
-                in_=xg[:, i * w * 4 : (i + 1) * w * 4],
+                out=xc[:, a * w : (a + 1) * w].bitcast(FP8X4),
+                scales=xs[:, a * w : (a + 1) * w],
+                in_=xg[:, a * w * 4 : (a + 1) * w * 4],
             )
-
-        def lora_mm(s):
-            j, i = divmod(s, NT)
-            lps[s] = []
-            for half in range(2):
-                lp = ps_l.tile([P, CH], F32, name="lp", tag="L")
-                nc.tensor.matmul(
-                    out=lp[:],
-                    lhsT=xat[:, i, :],
-                    rhs=b_sb[:, half, j * CH : (j + 1) * CH],
-                    start=True,
-                    stop=True,
-                )
-                lps[s].append(lp)
-
-        def lora_copy(s, half):
-            if half == 0:
-                e_new = epi.tile([P, 2, CH], F32, name="e", tag="e")
-                etiles[s] = e_new
-            nc.scalar.copy(out=etiles[s][:, half, :], in_=lps[s][half][:])
 
         def regroup(m):
             grp = wgrp.tile([P, 4 * CH], BF16, name="grp", tag="grp", align_bytes=64)
             grps[m] = grp
             dst = grp[:].rearrange("p (c i t) -> p c t i", i=4, t=4)
             src = raws[m][:].rearrange("p t (c i) -> p c t i", i=4)
-            vq = VCOLS_FIRST.get(m, VCOLS) // 4
+            vq = (VCOLS_EARLY if m < EARLY_TILES else VCOLS) // 4
             nc.vector.tensor_copy(out=dst[:, 0:vq], in_=src[:, 0:vq])
             if vq < CH // 4:
                 nc.scalar.copy(out=dst[:, vq : CH // 4], in_=src[:, vq : CH // 4])
+            if m + RAW_BUFS < NTILE:
+                load_w(m + RAW_BUFS)
 
         def w_quant(m):
             j, n = divmod(m, 2 * NG)
@@ -161,64 +150,99 @@ def tile_loramlp_pa_kernel(tc, x, xa, W_gate_up, B_gate_up, A_down, out_0, out_1
                 out=wc[:, half, g, :].bitcast(FP8X4), scales=ws[:, half, g, :], in_=grps[m][:]
             )
 
-        def mx(s):
-            j, i = divmod(s, NT)
+        def mx_transposed(u):
+            j, a = divmod(u, 2)
             wc, ws = wcodes[j]
-            mps[s] = []
+            mts[u] = []
             for half in range(2):
-                mp = ps_m.tile([P, CH], F32, name="mp", tag="M")
-                for g in range(NG):
-                    cols = slice((i * NG + g) * P, (i * NG + g + 1) * P)
-                    nc.tensor.matmul_mx(
-                        out=mp[:],
-                        lhsT=xc[:, cols].bitcast(FP8X4),
-                        lhsT_scale=xs[:, cols],
-                        rhs=wc[:, half, g, :].bitcast(FP8X4),
-                        rhs_scale=ws[:, half, g, :],
-                        start=(g == 0),
-                        stop=(g == NG - 1),
+                for qp in range(2):
+                    mt = ps_m.tile([P, 2, 2 * P], F32, name="mt", tag="M")
+                    for q2 in range(2):
+                        fcols = slice((2 * qp + q2) * P, (2 * qp + q2 + 1) * P)
+                        for g in range(NG):
+                            tcols = slice((a * NG + g) * 2 * P, (a * NG + g + 1) * 2 * P)
+                            nc.tensor.matmul_mx(
+                                out=mt[:, q2, :],
+                                lhsT=wc[:, half, g, fcols].bitcast(FP8X4),
+                                lhsT_scale=ws[:, half, g, fcols],
+                                rhs=xc[:, tcols].bitcast(FP8X4),
+                                rhs_scale=xs[:, tcols],
+                                start=(g == 0),
+                                stop=(g == NG - 1),
+                            )
+                    mts[u].append(mt)
+
+        def evacuate(u):
+            msbs[u] = []
+            for n in range(4):
+                ms = msp.tile([P, 2, 2 * P], F32, name="ms", tag="ms")
+                if u >= V_EVAC_FROM and n % 2 == 1:
+                    nc.vector.tensor_copy(out=ms[:], in_=mts[u][n][:])
+                else:
+                    nc.scalar.copy(out=ms[:], in_=mts[u][n][:])
+                msbs[u].append(ms)
+
+        def plain(u):
+            j, a = divmod(u, 2)
+            gus[u] = []
+            for b in range(2):
+                for half in range(2):
+                    gu = ps_m.tile([P, CH], F32, name="gu", tag="M")
+                    nc.tensor.matmul(
+                        out=gu[:],
+                        lhsT=xat[:, 2 * a + b, :],
+                        rhs=b_sb[:, half, j * CH : (j + 1) * CH],
+                        start=True,
+                        stop=False,
                     )
-                mps[s].append(mp)
+                    for q in range(4):
+                        nc.tensor.matmul(
+                            out=gu[:, q * P : (q + 1) * P],
+                            lhsT=msbs[u][2 * half + q // 2][:, q % 2, b * P : (b + 1) * P],
+                            rhs=ident_f[:],
+                            is_transpose=True,
+                            start=False,
+                            stop=(q == 3),
+                        )
+                    gus[u].append(gu)
 
-        def add(s, half):
-            e = etiles[s]
-            nc.vector.tensor_tensor(out=e[:, half, :], in0=mps[s][half][:], in1=e[:, half, :], op=ADD)
+        def silu(u, b):
+            e = epi.tile([P, 2, CH], F32, name="e", tag="e")
+            etiles[(u, b)] = e
+            nc.scalar.activation(out=e[:, 0, :], in_=gus[u][2 * b][:], func=SILU)
 
-        def silu(s):
-            e = etiles[s]
-            nc.scalar.activation(out=e[:, 0, :], in_=e[:, 0, :], func=SILU)
+        def mul(u, b):
+            e = etiles[(u, b)]
+            nc.vector.tensor_tensor(out=e[:, 1, :], in0=gus[u][2 * b + 1][:], in1=e[:, 0, :], op=MULT)
 
-        def mul(s):
-            e = etiles[s]
-            eng = nc.gpsimd if s < GPSIMD_MUL_STEPS else nc.vector
-            eng.tensor_tensor(out=e[:, 1, :], in0=e[:, 0, :], in1=e[:, 1, :], op=MULT)
-
-        def store(s):
-            j, i = divmod(s, NT)
+        def store(u, b):
+            j, a = divmod(u, 2)
+            i = 2 * a + b
             nc.sync.dma_start(
-                out=out_0[i * P : (i + 1) * P, j * CH : (j + 1) * CH], in_=etiles[s][:, 1, :]
+                out=out_0[i * P : (i + 1) * P, j * CH : (j + 1) * CH], in_=etiles[(u, b)][:, 1, :]
             )
 
-        def h_transpose(s):
+        def h_transpose(u, b):
             ht = ps_t.tile([P, 4, P], F32, name="ht", tag="T")
             for q in range(4):
                 nc.tensor.transpose(
-                    out=ht[:, q, :], in_=etiles[s][:, 1, q * P : (q + 1) * P], identity=ident_f[:]
+                    out=ht[:, q, :], in_=etiles[(u, b)][:, 1, q * P : (q + 1) * P], identity=ident_f[:]
                 )
-            hts[s] = ht
+            hts[(u, b)] = ht
 
-        def h_copy(s):
+        def h_copy(u, b):
             hg = hgp.tile([P, P, 4], BF16, name="hg", tag="hg", align_bytes=64)
-            nc.scalar.copy(out=hg[:], in_=hts[s][:].rearrange("p q t -> p t q"))
-            hgs[s] = hg
+            nc.scalar.copy(out=hg[:], in_=hts[(u, b)][:].rearrange("p q t -> p t q"))
+            hgs[(u, b)] = hg
 
-        def h_quant(s):
-            j, i = divmod(s, NT)
+        def h_quant(u, b):
+            j, a = divmod(u, 2)
+            i = 2 * a + b
             cols = slice(j * T + i * P, j * T + (i + 1) * P)
             nc.vector.quantize_mx(
                 out=hc[:, cols].bitcast(FP8X4),
                 scales=hs[:, cols],
-                in_=hgs[s][:].rearrange("p t q -> p (t q)"),
+                in_=hgs[(u, b)][:].rearrange("p t q -> p (t q)"),
             )
 
         def a_regroup(g):
@@ -250,70 +274,71 @@ def tile_loramlp_pa_kernel(tc, x, xa, W_gate_up, B_gate_up, A_down, out_0, out_1
             nc.scalar.copy(out=ha_sb[:, i, :], in_=ha_ps[:])
             nc.sync.dma_start(out=out_1[i * P : (i + 1) * P, :], in_=ha_sb[:, i, :])
 
+        warm = const.tile([P, 2], F32, name="warm")
+        nc.gpsimd.memset(warm[:, 0:1], 0.0)
+        nc.scalar.activation(out=warm[:, 1:2], in_=warm[:, 0:1], func=SILU)
+        xt0 = x_transpose(0)
+        xt1 = x_transpose(1)
+        x_copy(0, xt0, nc.vector.tensor_copy)
+        x_copy(1, xt1, nc.scalar.copy)
+        regroup(0)
+        x_quant(0)
+        regroup(1)
+        w_quant(0)
         xat_ps = ps_t.tile([P, NT, P], BF16, name="xat_ps", tag="T")
         for i in range(NT):
             nc.tensor.transpose(out=xat_ps[:, i, :], in_=xa_sb[:, i, :], identity=ident_b[:])
-        nc.vector.tensor_copy(out=xat[:], in_=xat_ps[:])
-        for s in range(4):
-            lora_mm(s)
-            lora_copy(s, 0)
-            lora_copy(s, 1)
-            if s == 1:
-                regroup(0)
-            if s == 2:
-                regroup(1)
-        w_quant(0)
-        w_quant(1)
-        x_copy(0, x_transpose(0), nc.vector.tensor_copy)
-        x_copy(1, x_transpose(1), nc.scalar.copy)
+        nc.scalar.copy(out=xat[:], in_=xat_ps[:])
         regroup(2)
-        x_quant(0)
-        x_copy(2, x_transpose(2), nc.scalar.copy)
-        x_copy(3, x_transpose(3), nc.scalar.copy)
+        w_quant(1)
         regroup(3)
         w_quant(2)
-        x_quant(1)
+        regroup(4)
         w_quant(3)
-        x_quant(2)
-        x_quant(3)
-        for m in range(RAW_BUFS, RAW_BUFS + 4):
-            load_w(m)
+        mx_transposed(0)
+        evacuate(0)
+        x_copy(2, x_transpose(2), nc.scalar.copy)
+        x_copy(3, x_transpose(3), nc.scalar.copy)
+        regroup(5)
+        w_quant(4)
+        x_quant(1)
+        regroup(6)
+        w_quant(5)
+        regroup(7)
 
-        for tick in range(-2, NSTEP + 4):
-            if 0 <= tick - 2 < NSTEP:
-                h_transpose(tick - 2)
-            if 0 <= tick + 1 < NSTEP:
-                mx(tick + 1)
-            if 0 <= tick < NSTEP:
-                add(tick, 0)
-                add(tick, 1)
-            if 4 <= tick + 3 < NSTEP:
-                lora_copy(tick + 3, 0)
-            if 0 <= tick < NSTEP:
-                silu(tick)
-            if 4 <= tick + 3 < NSTEP:
-                lora_copy(tick + 3, 1)
-            if 4 <= tick + 4 < NSTEP:
-                lora_mm(tick + 4)
-            if 0 <= tick - 1 < NSTEP:
-                mul(tick - 1)
-                if tick - 1 >= GPSIMD_MUL_STEPS:
-                    store(tick - 1)
-            if 0 <= tick - 2 < GPSIMD_MUL_STEPS:
-                store(tick - 2)
-            if 0 <= tick - 2 < NSTEP:
-                h_copy(tick - 2)
-            if 0 <= tick - 3 < NSTEP:
-                h_quant(tick - 3)
-            if 4 <= tick + 5 < NTILE:
-                w_quant(tick + 5)
-            if 4 <= tick + 6 < NTILE:
-                regroup(tick + 6)
-            if RAW_BUFS + 4 <= tick + 17 < NTILE:
-                load_w(tick + 17)
-            if 0 <= tick - 4 < NCH:
-                a_regroup(tick - 4)
-            if 0 <= tick - 5 < NCH:
-                a_quant(tick - 5)
-            if 0 <= tick - 3 - (NSTEP - NT) < NT:
-                second(tick - 3 - (NSTEP - NT))
+        for tau in range(0, NUNIT + 2):
+            if 0 <= tau - 1 < NUNIT:
+                for b in range(2):
+                    mul(tau - 1, b)
+                    store(tau - 1, b)
+            if 0 <= tau - 2 < NUNIT:
+                for b in range(2):
+                    h_copy(tau - 2, b)
+            if 0 <= tau + 1 < NUNIT:
+                mx_transposed(tau + 1)
+                evacuate(tau + 1)
+            if 0 <= tau < NUNIT:
+                plain(tau)
+                for b in range(2):
+                    silu(tau, b)
+            if 0 <= tau - 1 < NUNIT:
+                for b in range(2):
+                    h_transpose(tau - 1, b)
+            for m in (2 * tau + 6, 2 * tau + 7):
+                if m < NTILE:
+                    w_quant(m)
+            if 0 <= tau - 2 < NUNIT:
+                for b in range(2):
+                    h_quant(tau - 2, b)
+            for m in (2 * tau + 8, 2 * tau + 9):
+                if m < NTILE:
+                    regroup(m)
+            if tau == 6:
+                for g in range(NCH):
+                    a_regroup(g)
+            if tau == 7:
+                for g in range(NCH):
+                    a_quant(g)
+            if tau - 2 >= NUNIT - 2:
+                for b in range(2):
+                    second(2 * (tau - 2 - (NUNIT - 2)) + b)

@@ -195,16 +195,18 @@ def tile_loramlp_pa_kernel(tc, x, xa, W_gate_up, B_gate_up, A_down, out_0, out_1
                         start=True,
                         stop=False,
                     )
+                    gus[u].append(gu)
+            for b in range(2):
+                for half in range(2):
                     for q in range(4):
                         nc.tensor.matmul(
-                            out=gu[:, q * P : (q + 1) * P],
+                            out=gus[u][2 * b + half][:, q * P : (q + 1) * P],
                             lhsT=msbs[u][2 * half + q // 2][:, q % 2, b * P : (b + 1) * P],
                             rhs=ident_f[:],
                             is_transpose=True,
                             start=False,
                             stop=(q == 3),
                         )
-                    gus[u].append(gu)
 
         def silu(u, b):
             e = epi.tile([P, 2, CH], F32, name="e", tag="e")

@@ -22,7 +22,7 @@ NTILE = NCH * 2 * NG
 RAW_BUFS = 12
 EARLY_TILES = 8
 VCOLS_EARLY = 320
-VCOLS = 512
+VCOLS = 480
 V_EVAC_FROM = 7
 
 FLOPS = 2 * T * D * 2 * F + 2 * T * R * 2 * F + 2 * T * F * R
@@ -185,8 +185,8 @@ def tile_loramlp_pa_kernel(tc, x, xa, W_gate_up, B_gate_up, A_down, out_0, out_1
         def plain(u):
             j, a = divmod(u, 2)
             gus[u] = []
-            for b in range(2):
-                for half in range(2):
+            for half in range(2):
+                for b in range(2):
                     gu = ps_m.tile([P, CH], F32, name="gu", tag="M")
                     nc.tensor.matmul(
                         out=gu[:],
@@ -196,11 +196,11 @@ def tile_loramlp_pa_kernel(tc, x, xa, W_gate_up, B_gate_up, A_down, out_0, out_1
                         stop=False,
                     )
                     gus[u].append(gu)
-            for b in range(2):
-                for half in range(2):
+            for half in range(2):
+                for b in range(2):
                     for q in range(4):
                         nc.tensor.matmul(
-                            out=gus[u][2 * b + half][:, q * P : (q + 1) * P],
+                            out=gus[u][2 * half + b][:, q * P : (q + 1) * P],
                             lhsT=msbs[u][2 * half + q // 2][:, q % 2, b * P : (b + 1) * P],
                             rhs=ident_f[:],
                             is_transpose=True,
@@ -211,11 +211,11 @@ def tile_loramlp_pa_kernel(tc, x, xa, W_gate_up, B_gate_up, A_down, out_0, out_1
         def silu(u, b):
             e = epi.tile([P, 2, CH], F32, name="e", tag="e")
             etiles[(u, b)] = e
-            nc.scalar.activation(out=e[:, 0, :], in_=gus[u][2 * b][:], func=SILU)
+            nc.scalar.activation(out=e[:, 0, :], in_=gus[u][b][:], func=SILU)
 
         def mul(u, b):
             e = etiles[(u, b)]
-            nc.vector.tensor_tensor(out=e[:, 1, :], in0=gus[u][2 * b + 1][:], in1=e[:, 0, :], op=MULT)
+            nc.vector.tensor_tensor(out=e[:, 1, :], in0=gus[u][2 + b][:], in1=e[:, 0, :], op=MULT)
 
         def store(u, b):
             j, a = divmod(u, 2)

@@ -20,10 +20,9 @@ NCH = F // CH
 NUNIT = NCH * 2
 NTILE = NCH * 2 * NG
 RAW_BUFS = 12
-EARLY_TILES = 8
-VCOLS_EARLY = 320
-VCOLS = 480
-V_EVAC_FROM = 7
+VCOLS_HEAD = {0: 320, 1: 320, 2: 320, 3: 320, 4: 512, 5: 512, 6: 320, 7: 320}
+VCOLS = 448
+V_FREE_FROM = 7
 
 FLOPS = 2 * T * D * 2 * F + 2 * T * R * 2 * F + 2 * T * F * R
 
@@ -35,7 +34,7 @@ def tile_loramlp_pa_kernel(tc, x, xa, W_gate_up, B_gate_up, A_down, out_0, out_1
         wraw = ctx.enter_context(tc.tile_pool(name="wraw", bufs=RAW_BUFS))
         wgrp = ctx.enter_context(tc.tile_pool(name="wgrp", bufs=4))
         wcod = ctx.enter_context(tc.tile_pool(name="wcod", bufs=3))
-        msp = ctx.enter_context(tc.tile_pool(name="msp", bufs=8))
+        msp = ctx.enter_context(tc.tile_pool(name="msp", bufs=12))
         epi = ctx.enter_context(tc.tile_pool(name="epi", bufs=8))
         hgp = ctx.enter_context(tc.tile_pool(name="hgp", bufs=4))
         ps_m = ctx.enter_context(tc.psum_pool(name="ps_m", bufs=6))
@@ -50,6 +49,7 @@ def tile_loramlp_pa_kernel(tc, x, xa, W_gate_up, B_gate_up, A_down, out_0, out_1
         gus = {}
         etiles = {}
         hts = {}
+        has = {}
         hgs = {}
 
         def load_w(m):
@@ -72,14 +72,14 @@ def tile_loramlp_pa_kernel(tc, x, xa, W_gate_up, B_gate_up, A_down, out_0, out_1
         load_x(1)
         load_w(0)
         load_w(1)
+        load_x(2)
+        load_x(3)
+        load_w(2)
+        load_w(3)
         xa_sb = const.tile([P, NT, R], BF16, name="xa_sb")
         nc.sync.dma_start(out=xa_sb[:], in_=xa.rearrange("(i p) r -> p i r", p=P))
         b_sb = const.tile([P, 2, F], BF16, name="b_sb")
         b_view = B_gate_up.rearrange("r (h f) -> r h f", h=2)
-        load_w(2)
-        load_w(3)
-        load_x(2)
-        load_x(3)
         nc.sync.dma_start(out=b_sb[:, :, 0:CH], in_=b_view[:, :, 0:CH])
         for m in range(4, 8):
             load_w(m)
@@ -131,7 +131,7 @@ def tile_loramlp_pa_kernel(tc, x, xa, W_gate_up, B_gate_up, A_down, out_0, out_1
             grps[m] = grp
             dst = grp[:].rearrange("p (c i t) -> p c t i", i=4, t=4)
             src = raws[m][:].rearrange("p t (c i) -> p c t i", i=4)
-            vq = (VCOLS_EARLY if m < EARLY_TILES else VCOLS) // 4
+            vq = VCOLS_HEAD.get(m, VCOLS) // 4
             nc.vector.tensor_copy(out=dst[:, 0:vq], in_=src[:, 0:vq])
             if vq < CH // 4:
                 nc.scalar.copy(out=dst[:, vq : CH // 4], in_=src[:, vq : CH // 4])
@@ -150,11 +150,10 @@ def tile_loramlp_pa_kernel(tc, x, xa, W_gate_up, B_gate_up, A_down, out_0, out_1
                 out=wc[:, half, g, :].bitcast(FP8X4), scales=ws[:, half, g, :], in_=grps[m][:]
             )
 
-        def mx_transposed(u):
+        def mx_transposed(u, halves):
             j, a = divmod(u, 2)
             wc, ws = wcodes[j]
-            mts[u] = []
-            for half in range(2):
+            for half in halves:
                 for qp in range(2):
                     mt = ps_m.tile([P, 2, 2 * P], F32, name="mt", tag="M")
                     for q2 in range(2):
@@ -170,19 +169,16 @@ def tile_loramlp_pa_kernel(tc, x, xa, W_gate_up, B_gate_up, A_down, out_0, out_1
                                 start=(g == 0),
                                 stop=(g == NG - 1),
                             )
-                    mts[u].append(mt)
+                    mts[(u, 2 * half + qp)] = mt
 
-        def evacuate(u):
-            msbs[u] = []
-            for n in range(4):
-                ms = msp.tile([P, 2, 2 * P], F32, name="ms", tag="ms")
-                if u >= V_EVAC_FROM and n % 2 == 1:
-                    nc.vector.tensor_copy(out=ms[:], in_=mts[u][n][:])
-                else:
-                    nc.scalar.copy(out=ms[:], in_=mts[u][n][:])
-                msbs[u].append(ms)
+        def evacuate(u, halves):
+            for half in halves:
+                for qp in range(2):
+                    ms = msp.tile([P, 2, 2 * P], F32, name="ms", tag="ms")
+                    nc.scalar.copy(out=ms[:], in_=mts[(u, 2 * half + qp)][:])
+                    msbs[(u, 2 * half + qp)] = ms
 
-        def plain(u):
+        def lora_open(u):
             j, a = divmod(u, 2)
             gus[u] = []
             for half in range(2):
@@ -196,12 +192,14 @@ def tile_loramlp_pa_kernel(tc, x, xa, W_gate_up, B_gate_up, A_down, out_0, out_1
                         stop=False,
                     )
                     gus[u].append(gu)
+
+        def add_transposed(u):
             for half in range(2):
                 for b in range(2):
                     for q in range(4):
                         nc.tensor.matmul(
                             out=gus[u][2 * half + b][:, q * P : (q + 1) * P],
-                            lhsT=msbs[u][2 * half + q // 2][:, q % 2, b * P : (b + 1) * P],
+                            lhsT=msbs[(u, 2 * half + q // 2)][:, q % 2, b * P : (b + 1) * P],
                             rhs=ident_f[:],
                             is_transpose=True,
                             start=False,
@@ -232,9 +230,9 @@ def tile_loramlp_pa_kernel(tc, x, xa, W_gate_up, B_gate_up, A_down, out_0, out_1
                 )
             hts[(u, b)] = ht
 
-        def h_copy(u, b):
+        def h_copy(u, b, copy):
             hg = hgp.tile([P, P, 4], BF16, name="hg", tag="hg", align_bytes=64)
-            nc.scalar.copy(out=hg[:], in_=hts[(u, b)][:].rearrange("p q t -> p t q"))
+            copy(out=hg[:], in_=hts[(u, b)][:].rearrange("p q t -> p t q"))
             hgs[(u, b)] = hg
 
         def h_quant(u, b):
@@ -262,6 +260,7 @@ def tile_loramlp_pa_kernel(tc, x, xa, W_gate_up, B_gate_up, A_down, out_0, out_1
 
         def second(i):
             ha_ps = ps_m.tile([P, R], F32, name="ha_ps", tag="M")
+            has[i] = ha_ps
             for j in range(NCH):
                 cols = slice(j * T + i * P, j * T + (i + 1) * P)
                 nc.tensor.matmul_mx(
@@ -273,7 +272,9 @@ def tile_loramlp_pa_kernel(tc, x, xa, W_gate_up, B_gate_up, A_down, out_0, out_1
                     start=(j == 0),
                     stop=(j == NCH - 1),
                 )
-            nc.scalar.copy(out=ha_sb[:, i, :], in_=ha_ps[:])
+
+        def second_out(i, copy):
+            copy(out=ha_sb[:, i, :], in_=has[i][:])
             nc.sync.dma_start(out=out_1[i * P : (i + 1) * P, :], in_=ha_sb[:, i, :])
 
         warm = const.tile([P, 2], F32, name="warm")
@@ -281,66 +282,99 @@ def tile_loramlp_pa_kernel(tc, x, xa, W_gate_up, B_gate_up, A_down, out_0, out_1
         nc.scalar.activation(out=warm[:, 1:2], in_=warm[:, 0:1], func=SILU)
         xt0 = x_transpose(0)
         xt1 = x_transpose(1)
-        x_copy(0, xt0, nc.vector.tensor_copy)
+        x_copy(0, xt0, nc.scalar.copy)
         x_copy(1, xt1, nc.scalar.copy)
         regroup(0)
-        x_quant(0)
         regroup(1)
+        x_quant(0)
         w_quant(0)
+        w_quant(1)
+        xt2 = x_transpose(2)
+        xt3 = x_transpose(3)
+        x_copy(2, xt2, nc.scalar.copy)
+        x_copy(3, xt3, nc.scalar.copy)
+        regroup(2)
+        x_quant(1)
+        regroup(3)
+        mx_transposed(0, (0,))
+        mx_transposed(1, (0,))
+        w_quant(2)
+        w_quant(3)
+        evacuate(0, (0,))
+        evacuate(1, (0,))
         xat_ps = ps_t.tile([P, NT, P], BF16, name="xat_ps", tag="T")
         for i in range(NT):
             nc.tensor.transpose(out=xat_ps[:, i, :], in_=xa_sb[:, i, :], identity=ident_b[:])
         nc.scalar.copy(out=xat[:], in_=xat_ps[:])
-        regroup(2)
-        w_quant(1)
-        regroup(3)
-        w_quant(2)
+        mx_transposed(0, (1,))
+        mx_transposed(1, (1,))
+        evacuate(0, (1,))
+        evacuate(1, (1,))
         regroup(4)
-        w_quant(3)
-        mx_transposed(0)
-        evacuate(0)
-        x_copy(2, x_transpose(2), nc.scalar.copy)
-        x_copy(3, x_transpose(3), nc.scalar.copy)
         regroup(5)
         w_quant(4)
-        x_quant(1)
-        regroup(6)
         w_quant(5)
+        regroup(6)
         regroup(7)
+        lora_open(0)
+        add_transposed(0)
+        for b in range(2):
+            silu(0, b)
+        w_quant(6)
+        w_quant(7)
+        for b in range(2):
+            mul(0, b)
+            store(0, b)
+        regroup(8)
+        regroup(9)
 
-        for tau in range(0, NUNIT + 2):
-            if 0 <= tau - 1 < NUNIT:
+        for tau in range(1, NUNIT):
+            if tau >= 2:
                 for b in range(2):
                     mul(tau - 1, b)
                     store(tau - 1, b)
-            if 0 <= tau - 2 < NUNIT:
                 for b in range(2):
-                    h_copy(tau - 2, b)
-            if 0 <= tau + 1 < NUNIT:
-                mx_transposed(tau + 1)
-                evacuate(tau + 1)
-            if 0 <= tau < NUNIT:
-                plain(tau)
-                for b in range(2):
-                    silu(tau, b)
-            if 0 <= tau - 1 < NUNIT:
-                for b in range(2):
-                    h_transpose(tau - 1, b)
+                    h_quant(tau - 2, b)
+            if tau + 1 < NUNIT:
+                mx_transposed(tau + 1, (0, 1))
+                evacuate(tau + 1, (0, 1))
+            lora_open(tau)
+            for b in range(2):
+                h_transpose(tau - 1, b)
+                h_copy(tau - 1, b, nc.vector.tensor_copy if tau >= V_FREE_FROM else nc.scalar.copy)
+            add_transposed(tau)
+            for b in range(2):
+                silu(tau, b)
             for m in (2 * tau + 6, 2 * tau + 7):
                 if m < NTILE:
                     w_quant(m)
-            if 0 <= tau - 2 < NUNIT:
-                for b in range(2):
-                    h_quant(tau - 2, b)
             for m in (2 * tau + 8, 2 * tau + 9):
                 if m < NTILE:
                     regroup(m)
-            if tau == 6:
-                for g in range(NCH):
-                    a_regroup(g)
             if tau == 7:
                 for g in range(NCH):
+                    a_regroup(g)
+            if tau == 8:
+                for g in range(NCH):
                     a_quant(g)
-            if tau - 2 >= NUNIT - 2:
-                for b in range(2):
-                    second(2 * (tau - 2 - (NUNIT - 2)) + b)
+
+        last = NUNIT - 1
+        for b in range(2):
+            mul(last, b)
+            store(last, b)
+        for b in range(2):
+            h_quant(last - 1, b)
+        for b in range(2):
+            h_transpose(last, b)
+        h_copy(last, 0, nc.scalar.copy)
+        h_copy(last, 1, nc.vector.tensor_copy)
+        second(0)
+        second(1)
+        for b in range(2):
+            h_quant(last, b)
+        second(2)
+        second(3)
+        second_out(0, nc.scalar.copy)
+        second_out(1, nc.scalar.copy)
+        second_out(2, nc.scalar.copy)
+        second_out(3, nc.vector.tensor_copy)

@@ -8,6 +8,7 @@ BF16 = mybir.dt.bfloat16
 U32 = mybir.dt.uint32
 U8 = mybir.dt.uint8
 FP8X4 = mybir.dt.float8_e4m3fn_x4
+ADD = mybir.AluOpType.add
 MULT = mybir.AluOpType.mult
 SILU = mybir.ActivationFunctionType.Silu
 
@@ -22,7 +23,9 @@ NTILE = NCH * 2 * NG
 RAW_BUFS = 12
 VCOLS_HEAD = {0: 320, 1: 320, 2: 320, 3: 320, 4: 512, 5: 512, 6: 320, 7: 320}
 VCOLS = 448
-V_FREE_FROM = 7
+DIRECT_FROM = 7
+V_LORA_COPIES = ((1, 1),)
+GPSIMD_UNITS = (7, 8)
 
 FLOPS = 2 * T * D * 2 * F + 2 * T * R * 2 * F + 2 * T * F * R
 
@@ -36,7 +39,7 @@ def tile_loramlp_pa_kernel(tc, x, xa, W_gate_up, B_gate_up, A_down, out_0, out_1
         wcod = ctx.enter_context(tc.tile_pool(name="wcod", bufs=3))
         msp = ctx.enter_context(tc.tile_pool(name="msp", bufs=12))
         epi = ctx.enter_context(tc.tile_pool(name="epi", bufs=8))
-        hgp = ctx.enter_context(tc.tile_pool(name="hgp", bufs=4))
+        hgp = ctx.enter_context(tc.tile_pool(name="hgp", bufs=8))
         ps_m = ctx.enter_context(tc.psum_pool(name="ps_m", bufs=6))
         ps_t = ctx.enter_context(tc.psum_pool(name="ps_t", bufs=2))
         ctx.enter_context(tc.manual_schedule())
@@ -49,6 +52,8 @@ def tile_loramlp_pa_kernel(tc, x, xa, W_gate_up, B_gate_up, A_down, out_0, out_1
         gus = {}
         etiles = {}
         hts = {}
+        lps = {}
+        mps = {}
         has = {}
         hgs = {}
 
@@ -215,6 +220,59 @@ def tile_loramlp_pa_kernel(tc, x, xa, W_gate_up, B_gate_up, A_down, out_0, out_1
             e = etiles[(u, b)]
             nc.vector.tensor_tensor(out=e[:, 1, :], in0=gus[u][2 + b][:], in1=e[:, 0, :], op=MULT)
 
+        def lora_closed(u):
+            j, a = divmod(u, 2)
+            for b in range(2):
+                for half in range(2):
+                    lp = ps_m.tile([P, CH], F32, name="lp", tag="M")
+                    nc.tensor.matmul(
+                        out=lp[:],
+                        lhsT=xat[:, 2 * a + b, :],
+                        rhs=b_sb[:, half, j * CH : (j + 1) * CH],
+                        start=True,
+                        stop=True,
+                    )
+                    lps[(u, b, half)] = lp
+
+        def lora_copy(u, b, half):
+            if half == 0:
+                e_new = epi.tile([P, 2, CH], F32, name="e", tag="e")
+                etiles[(u, b)] = e_new
+            copy = nc.vector.tensor_copy if (b, half) in V_LORA_COPIES and u < NUNIT - 1 else nc.scalar.copy
+            copy(out=etiles[(u, b)][:, half, :], in_=lps[(u, b, half)][:])
+
+        def mx_direct(u):
+            j, a = divmod(u, 2)
+            wc, ws = wcodes[j]
+            for b in range(2):
+                for half in range(2):
+                    mp = ps_m.tile([P, CH], F32, name="mp", tag="M")
+                    for g in range(NG):
+                        tcols = slice(((a * NG + g) * 2 + b) * P, ((a * NG + g) * 2 + b + 1) * P)
+                        nc.tensor.matmul_mx(
+                            out=mp[:],
+                            lhsT=xc[:, tcols].bitcast(FP8X4),
+                            lhsT_scale=xs[:, tcols],
+                            rhs=wc[:, half, g, :].bitcast(FP8X4),
+                            rhs_scale=ws[:, half, g, :],
+                            start=(g == 0),
+                            stop=(g == NG - 1),
+                        )
+                    mps[(u, b, half)] = mp
+
+        def add(u, b, half):
+            e = etiles[(u, b)]
+            nc.vector.tensor_tensor(out=e[:, half, :], in0=mps[(u, b, half)][:], in1=e[:, half, :], op=ADD)
+
+        def silu_sb(u, b):
+            e = etiles[(u, b)]
+            nc.scalar.activation(out=e[:, 0, :], in_=e[:, 0, :], func=SILU)
+
+        def mul_sb(u, b):
+            e = etiles[(u, b)]
+            eng = nc.gpsimd if u in GPSIMD_UNITS else nc.vector
+            eng.tensor_tensor(out=e[:, 1, :], in0=e[:, 0, :], in1=e[:, 1, :], op=MULT)
+
         def store(u, b):
             j, a = divmod(u, 2)
             i = 2 * a + b
@@ -223,7 +281,10 @@ def tile_loramlp_pa_kernel(tc, x, xa, W_gate_up, B_gate_up, A_down, out_0, out_1
             )
 
         def h_transpose(u, b):
-            ht = ps_t.tile([P, 4, P], F32, name="ht", tag="T")
+            if u in (DIRECT_FROM, NUNIT - 1):
+                ht = ps_m.tile([P, 4, P], F32, name="ht2", tag="M")
+            else:
+                ht = ps_t.tile([P, 4, P], F32, name="ht", tag="T")
             for q in range(4):
                 nc.tensor.transpose(
                     out=ht[:, q, :], in_=etiles[(u, b)][:, 1, q * P : (q + 1) * P], identity=ident_f[:]
@@ -246,9 +307,13 @@ def tile_loramlp_pa_kernel(tc, x, xa, W_gate_up, B_gate_up, A_down, out_0, out_1
             )
 
         def a_regroup(g):
-            nc.vector.tensor_copy(
+            nc.gpsimd.tensor_scalar(
                 out=a_grp[:, g * R * 4 : (g + 1) * R * 4].rearrange("p (r t) -> p r t", t=4),
-                in_=a_raw[:, g * 4 : (g + 1) * 4, :].rearrange("p t r -> p r t"),
+                in0=a_raw[:, g * 4 : (g + 1) * 4, :].rearrange("p t r -> p r t"),
+                scalar1=1.0,
+                scalar2=0.0,
+                op0=MULT,
+                op1=ADD,
             )
 
         def a_quant(g):
@@ -258,10 +323,12 @@ def tile_loramlp_pa_kernel(tc, x, xa, W_gate_up, B_gate_up, A_down, out_0, out_1
                 in_=a_grp[:, g * R * 4 : (g + 1) * R * 4],
             )
 
-        def second(i):
-            ha_ps = ps_m.tile([P, R], F32, name="ha_ps", tag="M")
-            has[i] = ha_ps
-            for j in range(NCH):
+        def second(i, chunks):
+            if chunks[0] == 0:
+                ha_new = ps_m.tile([P, R], F32, name="ha_ps", tag="M")
+                has[i] = ha_new
+            ha_ps = has[i]
+            for j in chunks:
                 cols = slice(j * T + i * P, j * T + (i + 1) * P)
                 nc.tensor.matmul_mx(
                     out=ha_ps[:],
@@ -328,53 +395,85 @@ def tile_loramlp_pa_kernel(tc, x, xa, W_gate_up, B_gate_up, A_down, out_0, out_1
         regroup(8)
         regroup(9)
 
-        for tau in range(1, NUNIT):
+        def direct_stage(u):
+            lora_closed(u)
+            for b in range(2):
+                for half in range(2):
+                    lora_copy(u, b, half)
+            mx_direct(u)
+            for b in range(2):
+                add(u, b, 0)
+                add(u, b, 1)
+                silu_sb(u, b)
+
+        def product_direct(u):
+            for b in range(2):
+                mul_sb(u, b)
+                store(u, b)
+
+        def h_turn(u, copies):
+            for b in range(2):
+                h_transpose(u, b)
+                h_copy(u, b, copies[b])
+
+        S_COPY = nc.scalar.copy
+        V_COPY = nc.vector.tensor_copy
+
+        for tau in range(1, DIRECT_FROM):
             if tau >= 2:
                 for b in range(2):
                     mul(tau - 1, b)
                     store(tau - 1, b)
                 for b in range(2):
                     h_quant(tau - 2, b)
-            if tau + 1 < NUNIT:
+            if tau + 1 < DIRECT_FROM:
                 mx_transposed(tau + 1, (0, 1))
                 evacuate(tau + 1, (0, 1))
+            else:
+                direct_stage(tau + 1)
             lora_open(tau)
-            for b in range(2):
-                h_transpose(tau - 1, b)
-                h_copy(tau - 1, b, nc.vector.tensor_copy if tau >= V_FREE_FROM else nc.scalar.copy)
+            h_turn(tau - 1, (S_COPY, S_COPY))
             add_transposed(tau)
             for b in range(2):
                 silu(tau, b)
+            if tau + 1 == DIRECT_FROM:
+                product_direct(tau + 1)
+                for g in range(NCH):
+                    a_regroup(g)
             for m in (2 * tau + 6, 2 * tau + 7):
                 if m < NTILE:
                     w_quant(m)
             for m in (2 * tau + 8, 2 * tau + 9):
                 if m < NTILE:
                     regroup(m)
-            if tau == 7:
-                for g in range(NCH):
-                    a_regroup(g)
-            if tau == 8:
-                for g in range(NCH):
-                    a_quant(g)
 
-        last = NUNIT - 1
         for b in range(2):
-            mul(last, b)
-            store(last, b)
+            mul(6, b)
+            store(6, b)
         for b in range(2):
-            h_quant(last - 1, b)
+            h_quant(5, b)
+        direct_stage(8)
+        h_turn(6, (S_COPY, S_COPY))
+        for g in range(NCH):
+            a_quant(g)
+        h_turn(7, (V_COPY, V_COPY))
+        product_direct(8)
+        direct_stage(9)
+        product_direct(9)
+        h_turn(8, (S_COPY, S_COPY))
         for b in range(2):
-            h_transpose(last, b)
-        h_copy(last, 0, nc.scalar.copy)
-        h_copy(last, 1, nc.vector.tensor_copy)
-        second(0)
-        second(1)
+            h_quant(6, b)
+            h_quant(7, b)
+        h_turn(9, (S_COPY, V_COPY))
+        for i in range(NT):
+            second(i, range(NCH - 1))
         for b in range(2):
-            h_quant(last, b)
-        second(2)
-        second(3)
-        second_out(0, nc.scalar.copy)
-        second_out(1, nc.scalar.copy)
-        second_out(2, nc.scalar.copy)
-        second_out(3, nc.vector.tensor_copy)
+            h_quant(8, b)
+        for b in range(2):
+            h_quant(9, b)
+        for i in range(NT):
+            second(i, range(NCH - 1, NCH))
+        second_out(0, S_COPY)
+        second_out(1, V_COPY)
+        second_out(2, S_COPY)
+        second_out(3, V_COPY)

from contextlib import ExitStack

import concourse.mybir as mybir
from concourse.masks import make_identity

F32 = mybir.dt.float32
BF16 = mybir.dt.bfloat16
U32 = mybir.dt.uint32
U8 = mybir.dt.uint8
FP8X4 = mybir.dt.float8_e4m3fn_x4
ADD = mybir.AluOpType.add
MULT = mybir.AluOpType.mult
SILU = mybir.ActivationFunctionType.Silu

T, D, F, R = 512, 1024, 2560, 128
P = 128
NT = T // P
NG = D // 512
CH = 512
NCH = F // CH
NUNIT = NCH * 2
NTILE = NCH * 2 * NG
RAW_BUFS = 12
VCOLS_HEAD = {0: 320, 1: 320, 2: 320, 3: 320, 4: 512, 5: 512, 6: 320, 7: 320}
VCOLS = 448
DIRECT_FROM = 7
V_LORA_COPIES = ((1, 1),)
GPSIMD_UNITS = (7, 8)

FLOPS = 2 * T * D * 2 * F + 2 * T * R * 2 * F + 2 * T * F * R


def tile_loramlp_pa_kernel(tc, x, xa, W_gate_up, B_gate_up, A_down, out_0, out_1):
    nc = tc.nc
    with ExitStack() as ctx:
        const = ctx.enter_context(tc.tile_pool(name="const", bufs=1))
        wraw = ctx.enter_context(tc.tile_pool(name="wraw", bufs=RAW_BUFS))
        wgrp = ctx.enter_context(tc.tile_pool(name="wgrp", bufs=4))
        wcod = ctx.enter_context(tc.tile_pool(name="wcod", bufs=3))
        msp = ctx.enter_context(tc.tile_pool(name="msp", bufs=12))
        epi = ctx.enter_context(tc.tile_pool(name="epi", bufs=8))
        hgp = ctx.enter_context(tc.tile_pool(name="hgp", bufs=8))
        ps_m = ctx.enter_context(tc.psum_pool(name="ps_m", bufs=6))
        ps_t = ctx.enter_context(tc.psum_pool(name="ps_t", bufs=2))
        ctx.enter_context(tc.manual_schedule())

        raws = {}
        grps = {}
        wcodes = {}
        mts = {}
        msbs = {}
        gus = {}
        etiles = {}
        hts = {}
        lps = {}
        mps = {}
        has = {}
        hgs = {}

        def load_w(m):
            j, n = divmod(m, 2 * NG)
            half, g = divmod(n, NG)
            raw = wraw.tile([P, 4, CH], BF16, name="raw", tag="raw")
            c0 = half * F + j * CH
            nc.sync.dma_start(
                out=raw[:],
                in_=W_gate_up[g * 512 : (g + 1) * 512, c0 : c0 + CH].rearrange("(p t) c -> p t c", t=4),
            )
            raws[m] = raw

        x_sb = const.tile([P, NT * D], BF16, name="x_sb")

        def load_x(i):
            nc.sync.dma_start(out=x_sb[:, i * D : (i + 1) * D], in_=x[i * P : (i + 1) * P, :])

        load_x(0)
        load_x(1)
        load_w(0)
        load_w(1)
        load_x(2)
        load_x(3)
        load_w(2)
        load_w(3)
        xa_sb = const.tile([P, NT, R], BF16, name="xa_sb")
        nc.sync.dma_start(out=xa_sb[:], in_=xa.rearrange("(i p) r -> p i r", p=P))
        b_sb = const.tile([P, 2, F], BF16, name="b_sb")
        b_view = B_gate_up.rearrange("r (h f) -> r h f", h=2)
        nc.sync.dma_start(out=b_sb[:, :, 0:CH], in_=b_view[:, :, 0:CH])
        for m in range(4, 8):
            load_w(m)
        nc.sync.dma_start(out=b_sb[:, :, CH:F], in_=b_view[:, :, CH:F])
        for m in range(8, RAW_BUFS):
            load_w(m)
        a_raw = const.tile([P, NCH * 4, R], BF16, name="a_raw")
        nc.sync.dma_start(out=a_raw[:], in_=A_down.rearrange("(n p) r -> p n r", p=P))

        ident_f = const.tile([P, P], F32, name="ident_f")
        make_identity(nc, ident_f[:])
        ident_b = const.tile([P, P], BF16, name="ident_b")
        make_identity(nc, ident_b[:])

        xat = const.tile([P, NT, P], BF16, name="xat")
        xg = const.tile([P, NT * NG * P * 4], BF16, name="xg", align_bytes=64)
        xc = const.tile([P, NT * NG * P], U32, name="xc", align_bytes=64)
        xs = const.tile([P, NT * NG * P], U8, name="xs", align_bytes=64)
        hc = const.tile([P, NCH * T], U32, name="hc", align_bytes=64)
        hs = const.tile([P, NCH * T], U8, name="hs", align_bytes=64)
        a_grp = const.tile([P, NCH * R * 4], BF16, name="a_grp", align_bytes=64)
        ac = const.tile([P, NCH * R], U32, name="ac", align_bytes=64)
        a_s = const.tile([P, NCH * R], U8, name="a_s", align_bytes=64)
        ha_sb = const.tile([P, NT, R], F32, name="ha_sb")

        x_words = x_sb[:].bitcast(F32).rearrange("p (i g q u) -> p i g u q", i=NT, g=NG, u=2)
        xg_words = xg[:].bitcast(F32).rearrange("p (a g b t u) -> p a b g t u", a=2, g=NG, b=2, u=2)

        def x_transpose(i):
            xt = ps_t.tile([P, NG, 2, P], F32, name="xt", tag="T")
            for g in range(NG):
                for u in range(2):
                    nc.tensor.transpose(out=xt[:, g, u, :], in_=x_words[:, i, g, u, :], identity=ident_f[:])
            return xt

        def x_copy(i, xt, copy):
            copy(out=xg_words[:, i // 2, i % 2, :, :, :], in_=xt[:].rearrange("p g u t -> p g t u"))

        def x_quant(a):
            w = NG * 2 * P
            nc.vector.quantize_mx(
                out=xc[:, a * w : (a + 1) * w].bitcast(FP8X4),
                scales=xs[:, a * w : (a + 1) * w],
                in_=xg[:, a * w * 4 : (a + 1) * w * 4],
            )

        def regroup(m):
            grp = wgrp.tile([P, 4 * CH], BF16, name="grp", tag="grp", align_bytes=64)
            grps[m] = grp
            dst = grp[:].rearrange("p (c i t) -> p c t i", i=4, t=4)
            src = raws[m][:].rearrange("p t (c i) -> p c t i", i=4)
            vq = VCOLS_HEAD.get(m, VCOLS) // 4
            nc.vector.tensor_copy(out=dst[:, 0:vq], in_=src[:, 0:vq])
            if vq < CH // 4:
                nc.scalar.copy(out=dst[:, vq : CH // 4], in_=src[:, vq : CH // 4])
            if m + RAW_BUFS < NTILE:
                load_w(m + RAW_BUFS)

        def w_quant(m):
            j, n = divmod(m, 2 * NG)
            half, g = divmod(n, NG)
            if n == 0:
                wc_new = wcod.tile([P, 2, NG, CH], U32, name="wc", tag="wc", align_bytes=64)
                ws_new = wcod.tile([P, 2, NG, CH], U8, name="ws", tag="ws", align_bytes=64)
                wcodes[j] = (wc_new, ws_new)
            wc, ws = wcodes[j]
            nc.vector.quantize_mx(
                out=wc[:, half, g, :].bitcast(FP8X4), scales=ws[:, half, g, :], in_=grps[m][:]
            )

        def mx_transposed(u, halves):
            j, a = divmod(u, 2)
            wc, ws = wcodes[j]
            for half in halves:
                for qp in range(2):
                    mt = ps_m.tile([P, 2, 2 * P], F32, name="mt", tag="M")
                    for q2 in range(2):
                        fcols = slice((2 * qp + q2) * P, (2 * qp + q2 + 1) * P)
                        for g in range(NG):
                            tcols = slice((a * NG + g) * 2 * P, (a * NG + g + 1) * 2 * P)
                            nc.tensor.matmul_mx(
                                out=mt[:, q2, :],
                                lhsT=wc[:, half, g, fcols].bitcast(FP8X4),
                                lhsT_scale=ws[:, half, g, fcols],
                                rhs=xc[:, tcols].bitcast(FP8X4),
                                rhs_scale=xs[:, tcols],
                                start=(g == 0),
                                stop=(g == NG - 1),
                            )
                    mts[(u, 2 * half + qp)] = mt

        def evacuate(u, halves):
            for half in halves:
                for qp in range(2):
                    ms = msp.tile([P, 2, 2 * P], F32, name="ms", tag="ms")
                    nc.scalar.copy(out=ms[:], in_=mts[(u, 2 * half + qp)][:])
                    msbs[(u, 2 * half + qp)] = ms

        def lora_open(u):
            j, a = divmod(u, 2)
            gus[u] = []
            for half in range(2):
                for b in range(2):
                    gu = ps_m.tile([P, CH], F32, name="gu", tag="M")
                    nc.tensor.matmul(
                        out=gu[:],
                        lhsT=xat[:, 2 * a + b, :],
                        rhs=b_sb[:, half, j * CH : (j + 1) * CH],
                        start=True,
                        stop=False,
                    )
                    gus[u].append(gu)

        def add_transposed(u):
            for half in range(2):
                for b in range(2):
                    for q in range(4):
                        nc.tensor.matmul(
                            out=gus[u][2 * half + b][:, q * P : (q + 1) * P],
                            lhsT=msbs[(u, 2 * half + q // 2)][:, q % 2, b * P : (b + 1) * P],
                            rhs=ident_f[:],
                            is_transpose=True,
                            start=False,
                            stop=(q == 3),
                        )

        def silu(u, b):
            e = epi.tile([P, 2, CH], F32, name="e", tag="e")
            etiles[(u, b)] = e
            nc.scalar.activation(out=e[:, 0, :], in_=gus[u][b][:], func=SILU)

        def mul(u, b):
            e = etiles[(u, b)]
            nc.vector.tensor_tensor(out=e[:, 1, :], in0=gus[u][2 + b][:], in1=e[:, 0, :], op=MULT)

        def lora_closed(u):
            j, a = divmod(u, 2)
            for b in range(2):
                for half in range(2):
                    lp = ps_m.tile([P, CH], F32, name="lp", tag="M")
                    nc.tensor.matmul(
                        out=lp[:],
                        lhsT=xat[:, 2 * a + b, :],
                        rhs=b_sb[:, half, j * CH : (j + 1) * CH],
                        start=True,
                        stop=True,
                    )
                    lps[(u, b, half)] = lp

        def lora_copy(u, b, half):
            if half == 0:
                e_new = epi.tile([P, 2, CH], F32, name="e", tag="e")
                etiles[(u, b)] = e_new
            copy = nc.vector.tensor_copy if (b, half) in V_LORA_COPIES and u < NUNIT - 1 else nc.scalar.copy
            copy(out=etiles[(u, b)][:, half, :], in_=lps[(u, b, half)][:])

        def mx_direct(u):
            j, a = divmod(u, 2)
            wc, ws = wcodes[j]
            for b in range(2):
                for half in range(2):
                    mp = ps_m.tile([P, CH], F32, name="mp", tag="M")
                    for g in range(NG):
                        tcols = slice(((a * NG + g) * 2 + b) * P, ((a * NG + g) * 2 + b + 1) * P)
                        nc.tensor.matmul_mx(
                            out=mp[:],
                            lhsT=xc[:, tcols].bitcast(FP8X4),
                            lhsT_scale=xs[:, tcols],
                            rhs=wc[:, half, g, :].bitcast(FP8X4),
                            rhs_scale=ws[:, half, g, :],
                            start=(g == 0),
                            stop=(g == NG - 1),
                        )
                    mps[(u, b, half)] = mp

        def add(u, b, half):
            e = etiles[(u, b)]
            nc.vector.tensor_tensor(out=e[:, half, :], in0=mps[(u, b, half)][:], in1=e[:, half, :], op=ADD)

        def silu_sb(u, b):
            e = etiles[(u, b)]
            nc.scalar.activation(out=e[:, 0, :], in_=e[:, 0, :], func=SILU)

        def mul_sb(u, b):
            e = etiles[(u, b)]
            eng = nc.gpsimd if u in GPSIMD_UNITS else nc.vector
            eng.tensor_tensor(out=e[:, 1, :], in0=e[:, 0, :], in1=e[:, 1, :], op=MULT)

        def store(u, b):
            j, a = divmod(u, 2)
            i = 2 * a + b
            nc.sync.dma_start(
                out=out_0[i * P : (i + 1) * P, j * CH : (j + 1) * CH], in_=etiles[(u, b)][:, 1, :]
            )

        def h_transpose(u, b):
            if u in (DIRECT_FROM, NUNIT - 1):
                ht = ps_m.tile([P, 4, P], F32, name="ht2", tag="M")
            else:
                ht = ps_t.tile([P, 4, P], F32, name="ht", tag="T")
            for q in range(4):
                nc.tensor.transpose(
                    out=ht[:, q, :], in_=etiles[(u, b)][:, 1, q * P : (q + 1) * P], identity=ident_f[:]
                )
            hts[(u, b)] = ht

        def h_copy(u, b, copy):
            hg = hgp.tile([P, P, 4], BF16, name="hg", tag="hg", align_bytes=64)
            copy(out=hg[:], in_=hts[(u, b)][:].rearrange("p q t -> p t q"))
            hgs[(u, b)] = hg

        def h_quant(u, b):
            j, a = divmod(u, 2)
            i = 2 * a + b
            cols = slice(j * T + i * P, j * T + (i + 1) * P)
            nc.vector.quantize_mx(
                out=hc[:, cols].bitcast(FP8X4),
                scales=hs[:, cols],
                in_=hgs[(u, b)][:].rearrange("p t q -> p (t q)"),
            )

        def a_regroup(g):
            nc.gpsimd.tensor_scalar(
                out=a_grp[:, g * R * 4 : (g + 1) * R * 4].rearrange("p (r t) -> p r t", t=4),
                in0=a_raw[:, g * 4 : (g + 1) * 4, :].rearrange("p t r -> p r t"),
                scalar1=1.0,
                scalar2=0.0,
                op0=MULT,
                op1=ADD,
            )

        def a_quant(g):
            nc.vector.quantize_mx(
                out=ac[:, g * R : (g + 1) * R].bitcast(FP8X4),
                scales=a_s[:, g * R : (g + 1) * R],
                in_=a_grp[:, g * R * 4 : (g + 1) * R * 4],
            )

        def second(i, chunks):
            if chunks[0] == 0:
                ha_new = ps_m.tile([P, R], F32, name="ha_ps", tag="M")
                has[i] = ha_new
            ha_ps = has[i]
            for j in chunks:
                cols = slice(j * T + i * P, j * T + (i + 1) * P)
                nc.tensor.matmul_mx(
                    out=ha_ps[:],
                    lhsT=hc[:, cols].bitcast(FP8X4),
                    lhsT_scale=hs[:, cols],
                    rhs=ac[:, j * R : (j + 1) * R].bitcast(FP8X4),
                    rhs_scale=a_s[:, j * R : (j + 1) * R],
                    start=(j == 0),
                    stop=(j == NCH - 1),
                )

        def second_out(i, copy):
            copy(out=ha_sb[:, i, :], in_=has[i][:])
            nc.sync.dma_start(out=out_1[i * P : (i + 1) * P, :], in_=ha_sb[:, i, :])

        warm = const.tile([P, 2], F32, name="warm")
        nc.gpsimd.memset(warm[:, 0:1], 0.0)
        nc.scalar.activation(out=warm[:, 1:2], in_=warm[:, 0:1], func=SILU)
        xt0 = x_transpose(0)
        xt1 = x_transpose(1)
        x_copy(0, xt0, nc.scalar.copy)
        x_copy(1, xt1, nc.scalar.copy)
        regroup(0)
        regroup(1)
        x_quant(0)
        w_quant(0)
        w_quant(1)
        xt2 = x_transpose(2)
        xt3 = x_transpose(3)
        x_copy(2, xt2, nc.scalar.copy)
        x_copy(3, xt3, nc.scalar.copy)
        regroup(2)
        x_quant(1)
        regroup(3)
        mx_transposed(0, (0,))
        mx_transposed(1, (0,))
        w_quant(2)
        w_quant(3)
        evacuate(0, (0,))
        evacuate(1, (0,))
        xat_ps = ps_t.tile([P, NT, P], BF16, name="xat_ps", tag="T")
        for i in range(NT):
            nc.tensor.transpose(out=xat_ps[:, i, :], in_=xa_sb[:, i, :], identity=ident_b[:])
        nc.scalar.copy(out=xat[:], in_=xat_ps[:])
        mx_transposed(0, (1,))
        mx_transposed(1, (1,))
        evacuate(0, (1,))
        evacuate(1, (1,))
        regroup(4)
        regroup(5)
        w_quant(4)
        w_quant(5)
        regroup(6)
        regroup(7)
        lora_open(0)
        add_transposed(0)
        for b in range(2):
            silu(0, b)
        w_quant(6)
        w_quant(7)
        for b in range(2):
            mul(0, b)
            store(0, b)
        regroup(8)
        regroup(9)

        def direct_stage(u):
            lora_closed(u)
            for b in range(2):
                for half in range(2):
                    lora_copy(u, b, half)
            mx_direct(u)
            for b in range(2):
                add(u, b, 0)
                add(u, b, 1)
                silu_sb(u, b)

        def product_direct(u):
            for b in range(2):
                mul_sb(u, b)
                store(u, b)

        def h_turn(u, copies):
            for b in range(2):
                h_transpose(u, b)
                h_copy(u, b, copies[b])

        S_COPY = nc.scalar.copy
        V_COPY = nc.vector.tensor_copy

        for tau in range(1, DIRECT_FROM):
            if tau >= 2:
                for b in range(2):
                    mul(tau - 1, b)
                    store(tau - 1, b)
                for b in range(2):
                    h_quant(tau - 2, b)
            if tau + 1 < DIRECT_FROM:
                mx_transposed(tau + 1, (0, 1))
                evacuate(tau + 1, (0, 1))
            else:
                direct_stage(tau + 1)
            lora_open(tau)
            h_turn(tau - 1, (S_COPY, S_COPY))
            add_transposed(tau)
            for b in range(2):
                silu(tau, b)
            if tau + 1 == DIRECT_FROM:
                product_direct(tau + 1)
                for g in range(NCH):
                    a_regroup(g)
            for m in (2 * tau + 6, 2 * tau + 7):
                if m < NTILE:
                    w_quant(m)
            for m in (2 * tau + 8, 2 * tau + 9):
                if m < NTILE:
                    regroup(m)

        for b in range(2):
            mul(6, b)
            store(6, b)
        for b in range(2):
            h_quant(5, b)
        direct_stage(8)
        h_turn(6, (S_COPY, S_COPY))
        for g in range(NCH):
            a_quant(g)
        h_turn(7, (V_COPY, V_COPY))
        product_direct(8)
        direct_stage(9)
        product_direct(9)
        h_turn(8, (S_COPY, S_COPY))
        for b in range(2):
            h_quant(6, b)
            h_quant(7, b)
        h_turn(9, (S_COPY, V_COPY))
        for i in range(NT):
            second(i, range(NCH - 1))
        for b in range(2):
            h_quant(8, b)
        for b in range(2):
            h_quant(9, b)
        for i in range(NT):
            second(i, range(NCH - 1, NCH))
        second_out(0, S_COPY)
        second_out(1, V_COPY)
        second_out(2, S_COPY)
        second_out(3, V_COPY)
